import numpy as np
import ml_dtypes


def mxq(x, axis, fmt="e4m3"):
    dtype, down = {"e4m3": (ml_dtypes.float8_e4m3fn, 7), "e5m2": (ml_dtypes.float8_e5m2, 14)}[fmt]
    v = np.moveaxis(np.asarray(x, np.float32).astype(ml_dtypes.bfloat16).astype(np.float64), axis, -1)
    blocks = v.reshape(v.shape[:-1] + (-1, 32))
    amax = np.abs(blocks).max(-1, keepdims=True)
    byte = np.maximum(np.where(amax > 0, np.frexp(amax)[1] - 1 + 127, 0) - down, 1)
    scale = np.exp2(byte - 127.0)
    codes = (blocks / scale).astype(np.float32).astype(dtype).astype(np.float64)
    return np.moveaxis((codes * scale).reshape(v.shape), -1, axis)


WIDE = False


def mx_kscale(k):
    if not WIDE:
        return np.ones(k)
    levels = np.array([10, -10, 5, -5, 0])
    a = np.random.permutation(np.resize(levels, k // 512 * 4)).reshape(k // 512, 4)
    idx = np.arange(k)
    return np.exp2(a[idx // 512, idx % 128 // 32])


BF16 = ml_dtypes.bfloat16


def bf(x):
    return np.asarray(x, np.float32).astype(BF16)


def f64(x):
    return np.asarray(x).astype(np.float64)


N, NFEAT, NHID, NOUT, NCLS = 4096, 512, 128, 256, 128
C = NHID + NHID + NOUT
SPAN = 60.0
LAM = SPAN * np.log(2.0)


def log_softmax(v):
    v = v - v.max(axis=1, keepdims=True)
    return v - np.log(np.exp(v).sum(axis=1, keepdims=True))


def setup_inputs():
    t = mx_kscale(C)
    t1, t2, t3 = t[:NHID], t[NHID:NHID + NHID], t[NHID + NHID:]
    return {
        "x1": bf(np.maximum(np.random.standard_normal((N, NHID)), 0.0) * 0.75 * t1),
        "x2": bf(np.maximum(np.random.standard_normal((N, NHID)), 0.0) * t2),
        "adj": bf(np.exp2(-SPAN * np.random.uniform(size=(N, N))) * (LAM / N)),
        "W3": bf(np.random.standard_normal((NHID, NOUT)) * (1.4 / np.sqrt(NHID)) / t2[:, None] * t3),
        "b3": bf(np.random.standard_normal(NOUT) * 0.3 * t3),
        "Wl": bf(np.random.standard_normal((C, NCLS)) * (3.0 / np.sqrt(C)) / t[:, None]),
        "bl": bf(np.random.standard_normal(NCLS) * 0.3),
    }


def reference(x1, x2, adj, W3, b3, Wl, bl):
    support = f64(x2) @ f64(W3)
    x3 = (mxq(f64(adj), 1, "e4m3") @ mxq(support, 0, "e4m3")) + f64(b3)
    cat = np.concatenate((f64(x1), f64(x2), x3), axis=1)
    logits = (mxq(cat, 1, "e4m3") @ mxq(f64(Wl), 0, "e4m3")) + f64(bl)
    return log_softmax(logits)

@@ -1,0 +1,411 @@
+from contextlib import ExitStack
+
+import concourse.mybir as mybir
+from concourse.masks import make_identity
+
+F32 = mybir.dt.float32
+BF16 = mybir.dt.bfloat16
+U32 = mybir.dt.uint32
+U8 = mybir.dt.uint8
+FP8X4 = mybir.dt.float8_e4m3fn_x4
+ACT = mybir.ActivationFunctionType
+ALU = mybir.AluOpType
+AX = mybir.AxisListType
+
+P = 128
+NODES = 4096
+FLOPS = 2 * (NODES * 128 * 256 + NODES * NODES * 256 + NODES * 512 * 128)
+
+PINNED = True
+LAG = 2
+VE_EVEN = (2, 5)
+VE_ODD = ()
+VE_LAST = ()
+FIN_MOD = 2
+FIN_V = 1
+LN_AFTER = ()
+SL_RG = 1
+SL_CQ = 3
+SL_EXP = 2
+BLOCKS = [[0, 1], [2, 3], [4, 5], [6, 7], [8, 9], [10, 11], [12, 13], [14], [15]]
+
+
+def tile_gcn_pb_t_kernel(tc, x1, x2, adj, W3, b3, Wl, bl, out):
+    nc = tc.nc
+    adj_v = adj.rearrange("(a p e) j -> a p e j", p=P, e=2)
+    x1_v = x1.rearrange("(a p e) f -> p a e f", p=P, e=2)
+    x2_v = x2.rearrange("(a p e) f -> p a e f", p=P, e=2)
+    out_v = out.rearrange("(a p e) c -> p a e c", p=P, e=2)
+
+    with ExitStack() as ctx:
+        const = ctx.enter_context(tc.tile_pool(name="const", bufs=1))
+        big = ctx.enter_context(tc.tile_pool(name="big", bufs=5))
+        grp_pool = ctx.enter_context(tc.tile_pool(name="grp", bufs=6))
+        code_pool = ctx.enter_context(tc.tile_pool(name="code", bufs=2))
+        cat_pool = ctx.enter_context(tc.tile_pool(name="cat", bufs=2))
+        tp = ctx.enter_context(tc.psum_pool(name="tp", bufs=6))
+        accp = ctx.enter_context(tc.psum_pool(name="accp", bufs=2))
+        if PINNED:
+            ctx.enter_context(tc.manual_schedule())
+
+        zb = const.tile([P, P], BF16, name="zb")
+        yb = const.tile([P, P], BF16, name="yb")
+        ones = const.tile([P, P], BF16, name="ones")
+        dm = const.tile([P, 1], F32, name="dm")
+        dm2 = const.tile([P, 1], F32, name="dm2")
+        nc.vector.memset(zb[:], 0.0)
+        nc.vector.memset(yb[:], 0.0)
+        nc.vector.memset(ones[:], 1.0)
+        nc.vector.memset(dm[:], 0.0)
+        ident_b = const.tile([P, P], BF16, name="ident_b")
+        ident_f = const.tile([P, P], F32, name="ident_f")
+        make_identity(nc, ident_b[:])
+        make_identity(nc, ident_f[:])
+
+        wl_sb = const.tile([P, 4, P], BF16, name="wl_sb")
+        nc.scalar.dma_start(out=wl_sb[:], in_=Wl.rearrange("(t p) c -> p t c", p=P))
+        nc.scalar.dma_start(out=yb[0:2, :], in_=b3.rearrange("(h p) -> h p", h=2))
+        nc.scalar.dma_start(out=zb[0:1, :], in_=bl.rearrange("(o c) -> o c", o=1))
+        nc.scalar.activation(out=dm2[:], in_=dm[:], func=ACT.Exp)
+
+        w3 = const.tile([P, 256], BF16, name="w3")
+        nc.sync.dma_start(out=w3[:], in_=W3)
+        x12 = big.tile([P, 2, 16, 2, P], BF16, name="x12", tag="big", align_bytes=64)
+        for q in range(4):
+            nc.sync.dma_start(out=x12[:, 1, 4 * q:4 * q + 4], in_=x2_v[:, 4 * q:4 * q + 4])
+
+        raws = {}
+
+        def load(a):
+            raw = big.tile([P, 2, NODES], BF16, name="raw", tag="big", align_bytes=64)
+            nc.sync.dma_start(out=raw[:], in_=adj_v[a])
+            raws[a] = raw
+
+        load(0)
+        load(1)
+        nc.sync.dma_start(out=x12[:, 0], in_=x1_v)
+        load(2)
+
+        catp = const.tile([P, 4, NODES], BF16, name="catp")
+        logit = const.tile([P, 32, P], F32, name="logit")
+        negmax = const.tile([P, 32], F32, name="negmax")
+        sums = const.tile([P, 32], F32, name="sums")
+        lns = const.tile([P, 32], F32, name="lns")
+        shift = const.tile([P, 32], F32, name="shift")
+        junk = const.tile([P, P], BF16, name="junk")
+        b3c = const.tile([P, 2], F32, name="b3c")
+        blbc = const.tile([P, P], F32, name="blbc")
+        supc = const.tile([P, 16 * P], U32, name="supc", align_bytes=64)
+        sups = const.tile([P, 16 * P], U8, name="sups", align_bytes=64)
+        wlg = const.tile([P, P, 4], BF16, name="wlg", align_bytes=64)
+        wlc = const.tile([P, P], U32, name="wlc", align_bytes=64)
+        wls = const.tile([P, P], U8, name="wls", align_bytes=64)
+
+        flip = [0]
+
+        def copy_alt(dst, src):
+            flip[0] ^= 1
+            if flip[0]:
+                nc.scalar.copy(out=dst, in_=src)
+            else:
+                nc.vector.tensor_copy(out=dst, in_=src)
+
+        def feat_T(plane):
+            for q in range(8):
+                ps = tp.tile([P, 4, P], BF16, name="ps_x", tag="tp")
+                for j in range(4):
+                    tau = 4 * q + j
+                    nc.tensor.transpose(ps[:, j, :], x12[:, plane, tau // 2, tau % 2, :], ident_b[:])
+                copy_alt(catp[:, plane, 512 * q:512 * q + 512], ps[:].rearrange("p j n -> p (j n)"))
+
+        feat_T(1)
+
+        psb = tp.tile([P, P], BF16, name="psb", tag="tp")
+        nc.tensor.transpose(psb[:], yb[:], ident_b[:])
+        nc.vector.tensor_copy(out=b3c[:], in_=psb[:, 0:2])
+        psl = tp.tile([P, P], F32, name="psl", tag="tp")
+        nc.tensor.matmul(psl[:], lhsT=ones[:], rhs=zb[:], start=True, stop=True)
+        nc.vector.tensor_copy(out=blbc[:], in_=psl[:])
+
+        nc.vector.tensor_copy(
+            out=wlg[:].rearrange("p (c i) t -> p c t i", i=4),
+            in_=wl_sb[:].rearrange("p t (c i) -> p c t i", i=4),
+        )
+
+        supg = big.tile([P, 16, 512], BF16, name="supg", tag="big", align_bytes=64)
+
+        def sup_q(q):
+            nc.vector.quantize_mx(
+                out=supc[:, 512 * q:512 * q + 512].bitcast(FP8X4),
+                scales=sups[:, 512 * q:512 * q + 512],
+                in_=supg[:, 4 * q:4 * q + 4, :].rearrange("p s w -> p (s w)"),
+            )
+
+        for g in range(8):
+            for h in range(2):
+                ps = tp.tile([P, 4, P], F32, name="ps_s", tag="tp")
+                for t in range(4):
+                    nc.tensor.matmul(
+                        ps[:, t, :],
+                        lhsT=catp[:, 1, (4 * g + t) * P:(4 * g + t + 1) * P],
+                        rhs=w3[:, h * P:(h + 1) * P],
+                        start=True,
+                        stop=True,
+                    )
+                copy_alt(
+                    supg[:, 2 * g + h, :].rearrange("p (c t) -> p c t", t=4),
+                    ps[:].rearrange("p t c -> p c t"),
+                )
+                if g == 0 and h == 1:
+                    nc.vector.quantize_mx(out=wlc[:].bitcast(FP8X4), scales=wls[:], in_=wlg[:].rearrange("p c t -> p (c t)"))
+                if g % 2 == 0 and h == 1 and g >= 2:
+                    sup_q(g // 2 - 1)
+        sup_q(3)
+
+        blk_of = {}
+        for bi, tiles in enumerate(BLOCKS):
+            for hf, a in enumerate(tiles):
+                blk_of[a] = (bi, hf)
+        banks = {}
+        grps = {}
+        codes = {}
+        scls = {}
+        accs = {}
+        catcs = {}
+        lgs = {}
+
+        def T(a):
+            rawf = raws[a][:].bitcast(F32)
+            for g in range(8):
+                ps = tp.tile([P, 2, 256], F32, name="ps_t", tag="tp")
+                for u in range(2):
+                    for e in range(2):
+                        w0 = 256 * g + 128 * u
+                        nc.tensor.transpose(ps[:, u, e * P:(e + 1) * P], rawf[:, e, w0:w0 + P], ident_f[:])
+                banks[(a, g)] = ps
+
+        def E(a, g, on_vector):
+            ps = banks[(a, g)]
+            grp = grp_pool.tile([P, 1024], BF16, name="grp", align_bytes=64)
+            dst = grp[:].bitcast(F32).rearrange("p (n u) -> p n u", u=2)
+            src = ps[:].rearrange("p u n -> p n u")
+            if on_vector:
+                nc.vector.tensor_copy(out=dst, in_=src)
+            else:
+                nc.scalar.copy(out=dst, in_=src)
+            grps[(a, g)] = grp
+
+        def Q(a, g):
+            bi, hf = blk_of[a]
+            if bi not in codes:
+                n = 256 * len(BLOCKS[bi])
+                codes[bi] = code_pool.tile([P, 8, n], U32, name="codes", align_bytes=64)
+                scls[bi] = code_pool.tile([P, 8, n], U8, name="scls", align_bytes=64)
+            grp = grps[(a, g)]
+            nc.vector.quantize_mx(
+                out=codes[bi][:, g, 256 * hf:256 * hf + 256].bitcast(FP8X4),
+                scales=scls[bi][:, g, 256 * hf:256 * hf + 256],
+                in_=grp[:],
+            )
+
+        def EQ(a, ve, pieces):
+            for g in range(8):
+                E(a, g, g in ve)
+                if g >= LAG:
+                    Q(a, g - LAG)
+                for f in pieces.get(g, []):
+                    f()
+            for g in range(8 - LAG, 8):
+                Q(a, g)
+
+        def M(bi, gs):
+            n = 256 * len(BLOCKS[bi])
+            if bi not in accs:
+                acc0 = accp.tile([P, n], F32, name="acc0", tag="acc")
+                acc1 = accp.tile([P, n], F32, name="acc1", tag="acc")
+                accs[bi] = (acc0, acc1)
+            for g in gs:
+                for h in range(2):
+                    s0 = (2 * g + h) * P
+                    nc.tensor.matmul_mx(
+                        out=accs[bi][h][:],
+                        lhsT=supc[:, s0:s0 + P].bitcast(FP8X4),
+                        lhsT_scale=sups[:, s0:s0 + P],
+                        rhs=codes[bi][:, g, :].bitcast(FP8X4),
+                        rhs_scale=scls[bi][:, g, :],
+                        start=(g == 0),
+                        stop=(g == 7),
+                    )
+
+        def span(bi):
+            n0 = 256 * BLOCKS[bi][0]
+            return n0, 256 * len(BLOCKS[bi])
+
+        def X3E(bi):
+            n0, n = span(bi)
+            nc.scalar.activation(out=catp[:, 2, n0:n0 + n], in_=accs[bi][0][:], func=ACT.Identity, bias=b3c[:, 0:1], scale=1.0)
+            nc.vector.tensor_scalar(out=catp[:, 3, n0:n0 + n], in0=accs[bi][1][:], scalar1=b3c[:, 1:2], scalar2=None, op0=ALU.add)
+
+        def regroup(bi):
+            n0, n = span(bi)
+            catg = cat_pool.tile([P, n, 4], BF16, name="catg", align_bytes=64)
+            nc.vector.tensor_copy(
+                out=catg[:].rearrange("p (c i) t -> p c t i", i=4),
+                in_=catp[:, :, n0:n0 + n].rearrange("p t (c i) -> p c t i", i=4),
+            )
+            catcs[bi] = [catg]
+
+        def catQ(bi):
+            n0, n = span(bi)
+            catg = catcs[bi][0]
+            catc = cat_pool.tile([P, n], U32, name="catc", align_bytes=64)
+            cats = cat_pool.tile([P, n], U8, name="cats", align_bytes=64)
+            nc.vector.quantize_mx(out=catc[:].bitcast(FP8X4), scales=cats[:], in_=catg[:].rearrange("p n t -> p (n t)"))
+            catcs[bi] = [catc, cats]
+
+        def S3M(bi):
+            n0, n = span(bi)
+            nt = n // P
+            catc, cats = catcs[bi]
+            lg = tp.tile([P, nt, P], F32, name="lg", tag="tp")
+            for j in range(nt):
+                nc.tensor.matmul_mx(
+                    out=lg[:, j, :],
+                    lhsT=catc[:, j * P:(j + 1) * P].bitcast(FP8X4),
+                    lhsT_scale=cats[:, j * P:(j + 1) * P],
+                    rhs=wlc[:].bitcast(FP8X4),
+                    rhs_scale=wls[:],
+                    start=True,
+                    stop=True,
+                )
+            lgs[bi] = lg
+
+        def post_v(bi):
+            n0, n = span(bi)
+            nt = n // P
+            t0 = n0 // P
+            lb = logit[:, t0:t0 + nt, :]
+            nc.vector.tensor_tensor(out=lb, in0=lgs[bi][:], in1=blbc[:].unsqueeze(1).to_broadcast([P, nt, P]), op=ALU.add)
+            nc.vector.tensor_reduce(out=negmax[:, t0:t0 + nt], in_=lb, axis=AX.X, op=ALU.max, negate=True)
+
+        def post_s(bi):
+            n0, n = span(bi)
+            nt = n // P
+            t0 = n0 // P
+            for j in range(nt):
+                nc.scalar.activation(
+                    out=junk[:],
+                    in_=logit[:, t0 + j, :],
+                    func=ACT.Exp,
+                    bias=negmax[:, t0 + j:t0 + j + 1],
+                    scale=1.0,
+                    accum_out=sums[:, t0 + j:t0 + j + 1],
+                )
+
+        def ln_batch(t0, t1):
+            nc.scalar.activation(out=lns[:, t0:t1], in_=sums[:, t0:t1], func=ACT.Ln)
+            nc.vector.tensor_tensor(out=shift[:, t0:t1], in0=negmax[:, t0:t1], in1=lns[:, t0:t1], op=ALU.subtract)
+
+        def sub(t0, t1):
+            nc.vector.tensor_tensor(
+                out=logit[:, t0:t1, :],
+                in0=logit[:, t0:t1, :],
+                in1=shift[:, t0:t1].unsqueeze(2).to_broadcast([P, t1 - t0, P]),
+                op=ALU.add,
+            )
+
+        def sub_s(t0, t1):
+            for t in range(t0, t1):
+                nc.scalar.activation(out=logit[:, t, :], in_=logit[:, t, :], func=ACT.Identity, bias=shift[:, t:t + 1], scale=1.0)
+
+        def store(t0, t1):
+            nc.sync.dma_start(
+                out=out_v[:, t0 // 2:t1 // 2],
+                in_=logit[:, t0:t1, :].rearrange("p (a e) c -> p a e c", e=2),
+            )
+
+        late = []
+        late_i = [0]
+        done_t = [0]
+
+        def after_post(bi):
+            if bi in LN_AFTER:
+                n0, n = span(bi)
+                t1 = (n0 + n) // P
+                t0 = done_t[0]
+                ln_batch(t0, t1)
+                for s in range(t0, t1, 4):
+                    late.append((s, s + 4))
+                done_t[0] = t1
+
+        def next_sub():
+            if late_i[0] < len(late):
+                s0, s1 = late[late_i[0]]
+                late_i[0] += 1
+                sub(s0, s1)
+                store(s0, s1)
+
+        def odd_pieces(bi):
+            return {SL_RG: [lambda: regroup(bi)], SL_CQ: [lambda: catQ(bi)], 7: [next_sub]}
+
+        def even_pieces(bi):
+            if bi < 0:
+                return {}
+            return {SL_EXP: [lambda: post_s(bi), lambda: after_post(bi)], 7: [next_sub]}
+
+        T(0)
+        load(3)
+        EQ(0, VE_EVEN, {})
+        T(1)
+        EQ(1, VE_ODD, {})
+        feat_T(0)
+        load(4)
+        load(5)
+        load(6)
+        M(0, range(0, 4))
+        for a in range(2, 16):
+            T(a)
+            if a + 5 < 16:
+                load(a + 5)
+            if a % 2 == 0:
+                b = a // 2 - 1
+                EQ(a, VE_EVEN, even_pieces(b - 1))
+                M(b, range(4, 8))
+                X3E(b)
+            elif a < 15:
+                b = (a - 1) // 2
+                EQ(a, VE_ODD, odd_pieces(b - 1))
+                M(b, range(0, 4))
+                S3M(b - 1)
+                post_v(b - 1)
+            else:
+                EQ(a, VE_LAST, odd_pieces(6))
+        S3M(6)
+        M(7, range(8))
+        X3E(7)
+        post_v(6)
+        regroup(7)
+        catQ(7)
+        M(8, range(8))
+        X3E(8)
+        post_s(6)
+        regroup(8)
+        catQ(8)
+        S3M(7)
+        post_v(7)
+        post_s(7)
+        S3M(8)
+        post_v(8)
+        post_s(8)
+        for s0, s1 in late[late_i[0]:]:
+            sub(s0, s1)
+            store(s0, s1)
+        ln_batch(done_t[0], 32)
+        t = done_t[0]
+        while_t = list(range(done_t[0], 32, 2))
+        for i, t in enumerate(while_t):
+            if i % FIN_MOD < FIN_V:
+                sub(t, t + 2)
+            else:
+                sub_s(t, t + 2)
+            store(t, t + 2)

@@ -18,15 +18,14 @@ FLOPS = 2 * (NODES * 128 * 256 + NODES * NODES * 256 + NODES * 512 * 128)
 
 PINNED = True
 LAG = 2
-VE_EVEN = (2, 5)
-VE_ODD = ()
-VE_LAST = ()
+VE = {0: (2,), 1: (), 2: (2,), 3: ()}
+VE_TAIL = ()
 FIN_MOD = 2
 FIN_V = 1
-LN_AFTER = ()
-SL_RG = 1
-SL_CQ = 3
-SL_EXP = 2
+W_RG = (1, 0)
+W_CQ = (2, 0)
+W_S3M = 2
+W_EXP = (3, 2)
 BLOCKS = [[0, 1], [2, 3], [4, 5], [6, 7], [8, 9], [10, 11], [12, 13], [14], [15]]
 
 
@@ -39,7 +38,7 @@ def tile_gcn_pb_t_kernel(tc, x1, x2, adj, W3, b3, Wl, bl, out):
 
     with ExitStack() as ctx:
         const = ctx.enter_context(tc.tile_pool(name="const", bufs=1))
-        big = ctx.enter_context(tc.tile_pool(name="big", bufs=5))
+        big = ctx.enter_context(tc.tile_pool(name="big", bufs=4))
         grp_pool = ctx.enter_context(tc.tile_pool(name="grp", bufs=6))
         code_pool = ctx.enter_context(tc.tile_pool(name="code", bufs=2))
         cat_pool = ctx.enter_context(tc.tile_pool(name="cat", bufs=2))
@@ -70,7 +69,7 @@ def tile_gcn_pb_t_kernel(tc, x1, x2, adj, W3, b3, Wl, bl, out):
 
         w3 = const.tile([P, 256], BF16, name="w3")
         nc.sync.dma_start(out=w3[:], in_=W3)
-        x12 = big.tile([P, 2, 16, 2, P], BF16, name="x12", tag="big", align_bytes=64)
+        x12 = const.tile([P, 2, 16, 2, P], BF16, name="x12")
         for q in range(4):
             nc.sync.dma_start(out=x12[:, 1, 4 * q:4 * q + 4], in_=x2_v[:, 4 * q:4 * q + 4])
 
@@ -83,8 +82,8 @@ def tile_gcn_pb_t_kernel(tc, x1, x2, adj, W3, b3, Wl, bl, out):
 
         load(0)
         load(1)
-        nc.sync.dma_start(out=x12[:, 0], in_=x1_v)
         load(2)
+        nc.sync.dma_start(out=x12[:, 0], in_=x1_v)
 
         catp = const.tile([P, 4, NODES], BF16, name="catp")
         logit = const.tile([P, 32, P], F32, name="logit")
@@ -110,15 +109,15 @@ def tile_gcn_pb_t_kernel(tc, x1, x2, adj, W3, b3, Wl, bl, out):
             else:
                 nc.vector.tensor_copy(out=dst, in_=src)
 
-        def feat_T(plane):
-            for q in range(8):
+        def feat_T(plane, qs):
+            for q in qs:
                 ps = tp.tile([P, 4, P], BF16, name="ps_x", tag="tp")
                 for j in range(4):
                     tau = 4 * q + j
                     nc.tensor.transpose(ps[:, j, :], x12[:, plane, tau // 2, tau % 2, :], ident_b[:])
                 copy_alt(catp[:, plane, 512 * q:512 * q + 512], ps[:].rearrange("p j n -> p (j n)"))
 
-        feat_T(1)
+        feat_T(1, range(8))
 
         psb = tp.tile([P, P], BF16, name="psb", tag="tp")
         nc.tensor.transpose(psb[:], yb[:], ident_b[:])
@@ -174,9 +173,9 @@ def tile_gcn_pb_t_kernel(tc, x1, x2, adj, W3, b3, Wl, bl, out):
         catcs = {}
         lgs = {}
 
-        def T(a):
+        def T(a, gs):
             rawf = raws[a][:].bitcast(F32)
-            for g in range(8):
+            for g in gs:
                 ps = tp.tile([P, 2, 256], F32, name="ps_t", tag="tp")
                 for u in range(2):
                     for e in range(2):
@@ -208,34 +207,51 @@ def tile_gcn_pb_t_kernel(tc, x1, x2, adj, W3, b3, Wl, bl, out):
                 in_=grp[:],
             )
 
-        def EQ(a, ve, pieces):
-            for g in range(8):
-                E(a, g, g in ve)
-                if g >= LAG:
-                    Q(a, g - LAG)
-                for f in pieces.get(g, []):
-                    f()
-            for g in range(8 - LAG, 8):
+        pend = []
+        qi = [0]
+
+        def flush(keep):
+            for a, g in pend[qi[0]:len(pend) - keep]:
                 Q(a, g)
+            qi[0] = max(qi[0], len(pend) - keep)
+
+        def window(r, ve, pieces):
+            a = r // 2
+            for i in range(4):
+                g = 4 * (r % 2) + i
+                E(a, g, i in ve)
+                pend.append((a, g))
+                flush(LAG)
+                for f in pieces.get(i, []):
+                    f()
+
+        def mx(bi, g, h):
+            s0 = (2 * g + h) * P
+            nc.tensor.matmul_mx(
+                out=accs[bi][h],
+                lhsT=supc[:, s0:s0 + P].bitcast(FP8X4),
+                lhsT_scale=sups[:, s0:s0 + P],
+                rhs=codes[bi][:, g, :].bitcast(FP8X4),
+                rhs_scale=scls[bi][:, g, :],
+                start=(g == 0),
+                stop=(g == 7),
+            )
 
         def M(bi, gs):
-            n = 256 * len(BLOCKS[bi])
             if bi not in accs:
-                acc0 = accp.tile([P, n], F32, name="acc0", tag="acc")
-                acc1 = accp.tile([P, n], F32, name="acc1", tag="acc")
-                accs[bi] = (acc0, acc1)
+                acc0 = accp.tile([P, 512], F32, name="acc0", tag="acc")
+                acc1 = accp.tile([P, 512], F32, name="acc1", tag="acc")
+                accs[bi] = (acc0[:], acc1[:])
             for g in gs:
                 for h in range(2):
-                    s0 = (2 * g + h) * P
-                    nc.tensor.matmul_mx(
-                        out=accs[bi][h][:],
-                        lhsT=supc[:, s0:s0 + P].bitcast(FP8X4),
-                        lhsT_scale=sups[:, s0:s0 + P],
-                        rhs=codes[bi][:, g, :].bitcast(FP8X4),
-                        rhs_scale=scls[bi][:, g, :],
-                        start=(g == 0),
-                        stop=(g == 7),
-                    )
+                    mx(bi, g, h)
+
+        def M_small(bi):
+            acc = accp.tile([P, 2, 256], F32, name="acc", tag="acc")
+            accs[bi] = (acc[:, 0, :], acc[:, 1, :])
+            for h in range(2):
+                for g in range(8):
+                    mx(bi, g, h)
 
         def span(bi):
             n0 = 256 * BLOCKS[bi][0]
@@ -243,8 +259,8 @@ def tile_gcn_pb_t_kernel(tc, x1, x2, adj, W3, b3, Wl, bl, out):
 
         def X3E(bi):
             n0, n = span(bi)
-            nc.scalar.activation(out=catp[:, 2, n0:n0 + n], in_=accs[bi][0][:], func=ACT.Identity, bias=b3c[:, 0:1], scale=1.0)
-            nc.vector.tensor_scalar(out=catp[:, 3, n0:n0 + n], in0=accs[bi][1][:], scalar1=b3c[:, 1:2], scalar2=None, op0=ALU.add)
+            nc.scalar.activation(out=catp[:, 2, n0:n0 + n], in_=accs[bi][0], func=ACT.Identity, bias=b3c[:, 0:1], scale=1.0)
+            nc.vector.tensor_scalar(out=catp[:, 3, n0:n0 + n], in0=accs[bi][1], scalar1=b3c[:, 1:2], scalar2=None, op0=ALU.add)
 
         def regroup(bi):
             n0, n = span(bi)
@@ -302,10 +318,6 @@ def tile_gcn_pb_t_kernel(tc, x1, x2, adj, W3, b3, Wl, bl, out):
                     accum_out=sums[:, t0 + j:t0 + j + 1],
                 )
 
-        def ln_batch(t0, t1):
-            nc.scalar.activation(out=lns[:, t0:t1], in_=sums[:, t0:t1], func=ACT.Ln)
-            nc.vector.tensor_tensor(out=shift[:, t0:t1], in0=negmax[:, t0:t1], in1=lns[:, t0:t1], op=ALU.subtract)
-
         def sub(t0, t1):
             nc.vector.tensor_tensor(
                 out=logit[:, t0:t1, :],
@@ -324,70 +336,56 @@ def tile_gcn_pb_t_kernel(tc, x1, x2, adj, W3, b3, Wl, bl, out):
                 in_=logit[:, t0:t1, :].rearrange("p (a e) c -> p a e c", e=2),
             )
 
-        late = []
-        late_i = [0]
-        done_t = [0]
+        hung = {}
 
-        def after_post(bi):
-            if bi in LN_AFTER:
-                n0, n = span(bi)
-                t1 = (n0 + n) // P
-                t0 = done_t[0]
-                ln_batch(t0, t1)
-                for s in range(t0, t1, 4):
-                    late.append((s, s + 4))
-                done_t[0] = t1
+        def hang(r, i, f):
+            if r not in hung:
+                hung[r] = {}
+            if i not in hung[r]:
+                hung[r][i] = []
+            hung[r][i].append(f)
 
-        def next_sub():
-            if late_i[0] < len(late):
-                s0, s1 = late[late_i[0]]
-                late_i[0] += 1
-                sub(s0, s1)
-                store(s0, s1)
+        def plan(b):
+            r0 = 4 * b + 6
+            hang(r0 + W_RG[0], W_RG[1], lambda: regroup(b))
+            if b < 6:
+                hang(r0 + W_CQ[0], W_CQ[1], lambda: catQ(b))
+            if b < 5:
+                hang(r0 + W_EXP[0], W_EXP[1], lambda: post_s(b))
 
-        def odd_pieces(bi):
-            return {SL_RG: [lambda: regroup(bi)], SL_CQ: [lambda: catQ(bi)], 7: [next_sub]}
+        for b in range(7):
+            plan(b)
 
-        def even_pieces(bi):
-            if bi < 0:
-                return {}
-            return {SL_EXP: [lambda: post_s(bi), lambda: after_post(bi)], 7: [next_sub]}
-
-        T(0)
-        load(3)
-        EQ(0, VE_EVEN, {})
-        T(1)
-        EQ(1, VE_ODD, {})
-        feat_T(0)
-        load(4)
-        load(5)
-        load(6)
-        M(0, range(0, 4))
-        for a in range(2, 16):
-            T(a)
-            if a + 5 < 16:
-                load(a + 5)
-            if a % 2 == 0:
-                b = a // 2 - 1
-                EQ(a, VE_EVEN, even_pieces(b - 1))
-                M(b, range(4, 8))
-                X3E(b)
-            elif a < 15:
-                b = (a - 1) // 2
-                EQ(a, VE_ODD, odd_pieces(b - 1))
-                M(b, range(0, 4))
-                S3M(b - 1)
-                post_v(b - 1)
-            else:
-                EQ(a, VE_LAST, odd_pieces(6))
-        S3M(6)
-        M(7, range(8))
+        for r in range(32):
+            a = r // 2
+            T(a, range(4 * (r % 2), 4 * (r % 2) + 4))
+            if r % 4 == 2 and r >= 6:
+                feat_T(0, [(r - 6) // 4])
+            if r == 31:
+                feat_T(0, [7])
+            if r % 2 == 1 and a + 3 < 16 and a >= 0:
+                load(a + 3)
+            window(r, VE[r % 4] if r < 30 else VE_TAIL, hung.get(r, {}))
+            c = r - 3
+            if 0 <= c < 28:
+                M(c // 4, (2 * (c % 4), 2 * (c % 4) + 1))
+                if c % 4 == 3:
+                    X3E(c // 4)
+            bs = (r - 6 - W_S3M) // 4
+            if (r - 6 - W_S3M) % 4 == 0 and 0 <= bs < 7:
+                S3M(bs)
+                post_v(bs)
+        flush(0)
+        catQ(6)
+        M_small(7)
         X3E(7)
+        S3M(6)
         post_v(6)
         regroup(7)
         catQ(7)
-        M(8, range(8))
+        M_small(8)
         X3E(8)
+        post_s(5)
         post_s(6)
         regroup(8)
         catQ(8)
@@ -397,15 +395,11 @@ def tile_gcn_pb_t_kernel(tc, x1, x2, adj, W3, b3, Wl, bl, out):
         S3M(8)
         post_v(8)
         post_s(8)
-        for s0, s1 in late[late_i[0]:]:
-            sub(s0, s1)
-            store(s0, s1)
-        ln_batch(done_t[0], 32)
-        t = done_t[0]
-        while_t = list(range(done_t[0], 32, 2))
-        for i, t in enumerate(while_t):
+        nc.scalar.activation(out=lns[:], in_=sums[:], func=ACT.Ln)
+        nc.vector.tensor_tensor(out=shift[:], in0=negmax[:], in1=lns[:], op=ALU.subtract)
+        for i in range(16):
             if i % FIN_MOD < FIN_V:
-                sub(t, t + 2)
+                sub(2 * i, 2 * i + 2)
             else:
-                sub_s(t, t + 2)
-            store(t, t + 2)
+                sub_s(2 * i, 2 * i + 2)
+            store(2 * i, 2 * i + 2)

@@ -16,17 +16,18 @@ P = 128
 NODES = 4096
 FLOPS = 2 * (NODES * 128 * 256 + NODES * NODES * 256 + NODES * 512 * 128)
 
-PINNED = True
+NA = 16
 LAG = 2
-VE = {0: (2,), 1: (), 2: (2,), 3: ()}
-VE_TAIL = ()
-FIN_MOD = 2
-FIN_V = 1
-W_RG = (1, 0)
-W_CQ = (2, 0)
-W_S3M = 2
-W_EXP = (3, 2)
-BLOCKS = [[0, 1], [2, 3], [4, 5], [6, 7], [8, 9], [10, 11], [12, 13], [14], [15]]
+R = 3
+L = 22
+X1AT = {6 + 3 * q: (q,) for q in range(8)}
+VEM = 999
+H_RG = (1, 1)
+H_CQ = (2, 0)
+H_S3 = 3
+H_EX = (4, 2)
+WARM = 5
+SUP_HEAD = 5
 
 
 def tile_gcn_pb_t_kernel(tc, x1, x2, adj, W3, b3, Wl, bl, out):
@@ -40,18 +41,19 @@ def tile_gcn_pb_t_kernel(tc, x1, x2, adj, W3, b3, Wl, bl, out):
         const = ctx.enter_context(tc.tile_pool(name="const", bufs=1))
         big = ctx.enter_context(tc.tile_pool(name="big", bufs=4))
         grp_pool = ctx.enter_context(tc.tile_pool(name="grp", bufs=6))
-        code_pool = ctx.enter_context(tc.tile_pool(name="code", bufs=2))
+        code_pool = ctx.enter_context(tc.tile_pool(name="code", bufs=3))
         cat_pool = ctx.enter_context(tc.tile_pool(name="cat", bufs=2))
         tp = ctx.enter_context(tc.psum_pool(name="tp", bufs=6))
         accp = ctx.enter_context(tc.psum_pool(name="accp", bufs=2))
-        if PINNED:
-            ctx.enter_context(tc.manual_schedule())
+        ctx.enter_context(tc.manual_schedule())
 
         zb = const.tile([P, P], BF16, name="zb")
         yb = const.tile([P, P], BF16, name="yb")
         ones = const.tile([P, P], BF16, name="ones")
         dm = const.tile([P, 1], F32, name="dm")
         dm2 = const.tile([P, 1], F32, name="dm2")
+        warm = const.tile([P, 512], BF16, name="warm")
+        nc.vector.memset(warm[:], 0.0)
         nc.vector.memset(zb[:], 0.0)
         nc.vector.memset(yb[:], 0.0)
         nc.vector.memset(ones[:], 1.0)
@@ -117,7 +119,13 @@ def tile_gcn_pb_t_kernel(tc, x1, x2, adj, W3, b3, Wl, bl, out):
                     nc.tensor.transpose(ps[:, j, :], x12[:, plane, tau // 2, tau % 2, :], ident_b[:])
                 copy_alt(catp[:, plane, 512 * q:512 * q + 512], ps[:].rearrange("p j n -> p (j n)"))
 
-        feat_T(1, range(8))
+        def dummy(n):
+            ps = tp.tile([P, 512], F32, name="ps_d", tag="tp")
+            for i in range(n):
+                nc.tensor.matmul(ps[:], lhsT=warm[:, 0:P], rhs=warm[:], start=True, stop=True)
+
+        dummy(WARM)
+        feat_T(1, range(2))
 
         psb = tp.tile([P, P], BF16, name="psb", tag="tp")
         nc.tensor.transpose(psb[:], yb[:], ident_b[:])
@@ -140,7 +148,7 @@ def tile_gcn_pb_t_kernel(tc, x1, x2, adj, W3, b3, Wl, bl, out):
                 in_=supg[:, 4 * q:4 * q + 4, :].rearrange("p s w -> p (s w)"),
             )
 
-        for g in range(8):
+        def sup(g):
             for h in range(2):
                 ps = tp.tile([P, 4, P], F32, name="ps_s", tag="tp")
                 for t in range(4):
@@ -151,25 +159,26 @@ def tile_gcn_pb_t_kernel(tc, x1, x2, adj, W3, b3, Wl, bl, out):
                         start=True,
                         stop=True,
                     )
-                copy_alt(
+                (copy_alt if g < SUP_HEAD else nc.vector.tensor_copy)(
                     supg[:, 2 * g + h, :].rearrange("p (c t) -> p c t", t=4),
                     ps[:].rearrange("p t c -> p c t"),
                 )
-                if g == 0 and h == 1:
-                    nc.vector.quantize_mx(out=wlc[:].bitcast(FP8X4), scales=wls[:], in_=wlg[:].rearrange("p c t -> p (c t)"))
-                if g % 2 == 0 and h == 1 and g >= 2:
-                    sup_q(g // 2 - 1)
-        sup_q(3)
 
-        blk_of = {}
-        for bi, tiles in enumerate(BLOCKS):
-            for hf, a in enumerate(tiles):
-                blk_of[a] = (bi, hf)
+        for g in range(SUP_HEAD):
+            sup(g)
+            if g < 3:
+                feat_T(1, range(2 + 2 * g, 4 + 2 * g))
+            if g == 0:
+                nc.vector.quantize_mx(out=wlc[:].bitcast(FP8X4), scales=wls[:], in_=wlg[:].rearrange("p c t -> p (c t)"))
+            if g % 2 == 0 and g >= 2:
+                sup_q(g // 2 - 1)
+
         banks = {}
         grps = {}
         codes = {}
         scls = {}
         accs = {}
+        catgs = {}
         catcs = {}
         lgs = {}
 
@@ -184,10 +193,9 @@ def tile_gcn_pb_t_kernel(tc, x1, x2, adj, W3, b3, Wl, bl, out):
                 banks[(a, g)] = ps
 
         def E(a, g, on_vector):
-            ps = banks[(a, g)]
             grp = grp_pool.tile([P, 1024], BF16, name="grp", align_bytes=64)
             dst = grp[:].bitcast(F32).rearrange("p (n u) -> p n u", u=2)
-            src = ps[:].rearrange("p u n -> p n u")
+            src = banks[(a, g)][:].rearrange("p u n -> p n u")
             if on_vector:
                 nc.vector.tensor_copy(out=dst, in_=src)
             else:
@@ -195,16 +203,13 @@ def tile_gcn_pb_t_kernel(tc, x1, x2, adj, W3, b3, Wl, bl, out):
             grps[(a, g)] = grp
 
         def Q(a, g):
-            bi, hf = blk_of[a]
-            if bi not in codes:
-                n = 256 * len(BLOCKS[bi])
-                codes[bi] = code_pool.tile([P, 8, n], U32, name="codes", align_bytes=64)
-                scls[bi] = code_pool.tile([P, 8, n], U8, name="scls", align_bytes=64)
-            grp = grps[(a, g)]
+            if a not in codes:
+                codes[a] = code_pool.tile([P, 8, 256], U32, name="codes", align_bytes=64)
+                scls[a] = code_pool.tile([P, 8, 256], U8, name="scls", align_bytes=64)
             nc.vector.quantize_mx(
-                out=codes[bi][:, g, 256 * hf:256 * hf + 256].bitcast(FP8X4),
-                scales=scls[bi][:, g, 256 * hf:256 * hf + 256],
-                in_=grp[:],
+                out=codes[a][:, g, :].bitcast(FP8X4),
+                scales=scls[a][:, g, :],
+                in_=grps[(a, g)][:],
             )
 
         pend = []
@@ -215,78 +220,47 @@ def tile_gcn_pb_t_kernel(tc, x1, x2, adj, W3, b3, Wl, bl, out):
                 Q(a, g)
             qi[0] = max(qi[0], len(pend) - keep)
 
-        def window(r, ve, pieces):
-            a = r // 2
-            for i in range(4):
-                g = 4 * (r % 2) + i
-                E(a, g, i in ve)
-                pend.append((a, g))
-                flush(LAG)
-                for f in pieces.get(i, []):
-                    f()
-
-        def mx(bi, g, h):
+        def M(m):
+            a, h, g = m // 16, m % 16 // 8, m % 8
+            if h == 0 and g == 0:
+                accs[a] = accp.tile([P, 2, 256], F32, name="acc")
             s0 = (2 * g + h) * P
             nc.tensor.matmul_mx(
-                out=accs[bi][h],
+                out=accs[a][:, h, :],
                 lhsT=supc[:, s0:s0 + P].bitcast(FP8X4),
                 lhsT_scale=sups[:, s0:s0 + P],
-                rhs=codes[bi][:, g, :].bitcast(FP8X4),
-                rhs_scale=scls[bi][:, g, :],
+                rhs=codes[a][:, g, :].bitcast(FP8X4),
+                rhs_scale=scls[a][:, g, :],
                 start=(g == 0),
                 stop=(g == 7),
             )
 
-        def M(bi, gs):
-            if bi not in accs:
-                acc0 = accp.tile([P, 512], F32, name="acc0", tag="acc")
-                acc1 = accp.tile([P, 512], F32, name="acc1", tag="acc")
-                accs[bi] = (acc0[:], acc1[:])
-            for g in gs:
-                for h in range(2):
-                    mx(bi, g, h)
+        def X3E(a):
+            n0 = 256 * a
+            nc.scalar.activation(out=catp[:, 2, n0:n0 + 256], in_=accs[a][:, 0, :], func=ACT.Identity, bias=b3c[:, 0:1], scale=1.0)
+            nc.vector.tensor_scalar(out=catp[:, 3, n0:n0 + 256], in0=accs[a][:, 1, :], scalar1=b3c[:, 1:2], scalar2=None, op0=ALU.add)
 
-        def M_small(bi):
-            acc = accp.tile([P, 2, 256], F32, name="acc", tag="acc")
-            accs[bi] = (acc[:, 0, :], acc[:, 1, :])
-            for h in range(2):
-                for g in range(8):
-                    mx(bi, g, h)
-
-        def span(bi):
-            n0 = 256 * BLOCKS[bi][0]
-            return n0, 256 * len(BLOCKS[bi])
-
-        def X3E(bi):
-            n0, n = span(bi)
-            nc.scalar.activation(out=catp[:, 2, n0:n0 + n], in_=accs[bi][0], func=ACT.Identity, bias=b3c[:, 0:1], scale=1.0)
-            nc.vector.tensor_scalar(out=catp[:, 3, n0:n0 + n], in0=accs[bi][1], scalar1=b3c[:, 1:2], scalar2=None, op0=ALU.add)
-
-        def regroup(bi):
-            n0, n = span(bi)
-            catg = cat_pool.tile([P, n, 4], BF16, name="catg", align_bytes=64)
+        def regroup(a):
+            n0 = 256 * a
+            catg = cat_pool.tile([P, 256, 4], BF16, name="catg", align_bytes=64)
             nc.vector.tensor_copy(
                 out=catg[:].rearrange("p (c i) t -> p c t i", i=4),
-                in_=catp[:, :, n0:n0 + n].rearrange("p t (c i) -> p c t i", i=4),
+                in_=catp[:, :, n0:n0 + 256].rearrange("p t (c i) -> p c t i", i=4),
             )
-            catcs[bi] = [catg]
+            catgs[a] = catg
 
-        def catQ(bi):
-            n0, n = span(bi)
-            catg = catcs[bi][0]
-            catc = cat_pool.tile([P, n], U32, name="catc", align_bytes=64)
-            cats = cat_pool.tile([P, n], U8, name="cats", align_bytes=64)
-            nc.vector.quantize_mx(out=catc[:].bitcast(FP8X4), scales=cats[:], in_=catg[:].rearrange("p n t -> p (n t)"))
-            catcs[bi] = [catc, cats]
+        def catQ(a):
+            catc = cat_pool.tile([P, 256], U32, name="catc", align_bytes=64)
+            cats = cat_pool.tile([P, 256], U8, name="cats", align_bytes=64)
+            nc.vector.quantize_mx(out=catc[:].bitcast(FP8X4), scales=cats[:], in_=catgs[a][:].rearrange("p n t -> p (n t)"))
+            catcs[a] = (catc, cats)
 
-        def S3M(bi):
-            n0, n = span(bi)
-            nt = n // P
-            catc, cats = catcs[bi]
-            lg = tp.tile([P, nt, P], F32, name="lg", tag="tp")
-            for j in range(nt):
+        def S3M(a):
+            catc, cats = catcs[a]
+            lgs[a] = tp.tile([P, 2, P], F32, name="lg", tag="tp")
+            for j in range(2):
                 nc.tensor.matmul_mx(
-                    out=lg[:, j, :],
+                    out=lgs[a][:, j, :],
                     lhsT=catc[:, j * P:(j + 1) * P].bitcast(FP8X4),
                     lhsT_scale=cats[:, j * P:(j + 1) * P],
                     rhs=wlc[:].bitcast(FP8X4),
@@ -294,37 +268,32 @@ def tile_gcn_pb_t_kernel(tc, x1, x2, adj, W3, b3, Wl, bl, out):
                     start=True,
                     stop=True,
                 )
-            lgs[bi] = lg
 
-        def post_v(bi):
-            n0, n = span(bi)
-            nt = n // P
-            t0 = n0 // P
-            lb = logit[:, t0:t0 + nt, :]
-            nc.vector.tensor_tensor(out=lb, in0=lgs[bi][:], in1=blbc[:].unsqueeze(1).to_broadcast([P, nt, P]), op=ALU.add)
-            nc.vector.tensor_reduce(out=negmax[:, t0:t0 + nt], in_=lb, axis=AX.X, op=ALU.max, negate=True)
+        def post_v(a):
+            lb = logit[:, 2 * a:2 * a + 2, :]
+            nc.vector.tensor_tensor(out=lb, in0=lgs[a][:], in1=blbc[:].unsqueeze(1).to_broadcast([P, 2, P]), op=ALU.add)
+            nc.vector.tensor_reduce(out=negmax[:, 2 * a:2 * a + 2], in_=lb, axis=AX.X, op=ALU.max, negate=True)
 
-        def post_s(bi):
-            n0, n = span(bi)
-            nt = n // P
-            t0 = n0 // P
-            for j in range(nt):
+        def post_s(a):
+            for t in range(2 * a, 2 * a + 2):
                 nc.scalar.activation(
                     out=junk[:],
-                    in_=logit[:, t0 + j, :],
+                    in_=logit[:, t, :],
                     func=ACT.Exp,
-                    bias=negmax[:, t0 + j:t0 + j + 1],
+                    bias=negmax[:, t:t + 1],
                     scale=1.0,
-                    accum_out=sums[:, t0 + j:t0 + j + 1],
+                    accum_out=sums[:, t:t + 1],
                 )
 
+        def logs(t0, t1):
+            nc.scalar.activation(out=lns[:, t0:t1], in_=sums[:, t0:t1], func=ACT.Ln)
+            nc.vector.tensor_tensor(out=shift[:, t0:t1], in0=negmax[:, t0:t1], in1=lns[:, t0:t1], op=ALU.subtract)
+
         def sub(t0, t1):
-            nc.vector.tensor_tensor(
-                out=logit[:, t0:t1, :],
-                in0=logit[:, t0:t1, :],
-                in1=shift[:, t0:t1].unsqueeze(2).to_broadcast([P, t1 - t0, P]),
-                op=ALU.add,
-            )
+            for t in range(t0, t1):
+                nc.vector.tensor_scalar(
+                    out=logit[:, t, :], in0=logit[:, t, :], scalar1=shift[:, t:t + 1], scalar2=None, op0=ALU.add
+                )
 
         def sub_s(t0, t1):
             for t in range(t0, t1):
@@ -336,70 +305,68 @@ def tile_gcn_pb_t_kernel(tc, x1, x2, adj, W3, b3, Wl, bl, out):
                 in_=logit[:, t0:t1, :].rearrange("p (a e) c -> p a e c", e=2),
             )
 
+        def fin(t):
+            if t // 2 % 5 in (0, 2, 4):
+                sub(t, t + 2)
+            else:
+                sub_s(t, t + 2)
+            store(t, t + 2)
+
         hung = {}
 
         def hang(r, i, f):
-            if r not in hung:
-                hung[r] = {}
-            if i not in hung[r]:
-                hung[r][i] = []
-            hung[r][i].append(f)
+            hung.setdefault(r, {}).setdefault(i, []).append(f)
 
-        def plan(b):
-            r0 = 4 * b + 6
-            hang(r0 + W_RG[0], W_RG[1], lambda: regroup(b))
-            if b < 6:
-                hang(r0 + W_CQ[0], W_CQ[1], lambda: catQ(b))
-            if b < 5:
-                hang(r0 + W_EXP[0], W_EXP[1], lambda: post_s(b))
-
-        for b in range(7):
-            plan(b)
-
-        for r in range(32):
-            a = r // 2
-            T(a, range(4 * (r % 2), 4 * (r % 2) + 4))
-            if r % 4 == 2 and r >= 6:
-                feat_T(0, [(r - 6) // 4])
-            if r == 31:
-                feat_T(0, [7])
-            if r % 2 == 1 and a + 3 < 16 and a >= 0:
-                load(a + 3)
-            window(r, VE[r % 4] if r < 30 else VE_TAIL, hung.get(r, {}))
-            c = r - 3
-            if 0 <= c < 28:
-                M(c // 4, (2 * (c % 4), 2 * (c % 4) + 1))
-                if c % 4 == 3:
-                    X3E(c // 4)
-            bs = (r - 6 - W_S3M) // 4
-            if (r - 6 - W_S3M) % 4 == 0 and 0 <= bs < 7:
-                S3M(bs)
-                post_v(bs)
-        flush(0)
-        catQ(6)
-        M_small(7)
-        X3E(7)
-        S3M(6)
-        post_v(6)
-        regroup(7)
-        catQ(7)
-        M_small(8)
-        X3E(8)
-        post_s(5)
-        post_s(6)
-        regroup(8)
-        catQ(8)
-        S3M(7)
-        post_v(7)
-        post_s(7)
-        S3M(8)
-        post_v(8)
-        post_s(8)
-        nc.scalar.activation(out=lns[:], in_=sums[:], func=ACT.Ln)
-        nc.vector.tensor_tensor(out=shift[:], in0=negmax[:], in1=lns[:], op=ALU.subtract)
-        for i in range(16):
-            if i % FIN_MOD < FIN_V:
-                sub(2 * i, 2 * i + 2)
-            else:
-                sub_s(2 * i, 2 * i + 2)
-            store(2 * i, 2 * i + 2)
+        units = [(a, g) for a in range(NA) for g in range(8)]
+        nruns = -(-len(units) // R)
+        md = [0]
+        ends = {}
+        for j in range(nruns + 99):
+            us = units[R * j:R * j + R]
+            for a, g in us:
+                T(a, (g,))
+                if g == 7 and a + 3 < NA:
+                    load(a + 3)
+            for q in X1AT.get(j, ()):
+                feat_T(0, (q,))
+            if SUP_HEAD + j < 8:
+                sup(SUP_HEAD + j)
+            pieces = hung.get(j, {})
+            if not us:
+                flush(0)
+            for i in range(max(R, 4)):
+                if i < len(us):
+                    a, g = us[i]
+                    E(a, g, (R * j + i) % VEM == 1 and j >= 6)
+                    pend.append((a, g))
+                    flush(LAG)
+                for f in pieces.get(i, []):
+                    f()
+            if SUP_HEAD + j == 6:
+                sup_q(2)
+            if SUP_HEAD + j == 7:
+                sup_q(3)
+            target = min(256, 2 * R * (j + 1) - L)
+            while md[0] < target:
+                m = md[0]
+                M(m)
+                md[0] += 1
+                if m % 16 == 15:
+                    a = m // 16
+                    X3E(a)
+                    hang(j + H_RG[0], H_RG[1], lambda a=a: regroup(a))
+                    hang(j + H_CQ[0], H_CQ[1], lambda a=a: catQ(a))
+                    if a < NA - 2:
+                        hang(j + H_EX[0], H_EX[1], lambda a=a: post_s(a))
+                    ends[a] = j + H_S3
+            for a in list(ends):
+                if ends[a] == j:
+                    S3M(a)
+                    post_v(a)
+            if target == 256 and ends[NA - 1] == j:
+                break
+        for a in range(NA - 2, NA):
+            post_s(a)
+        logs(0, 32)
+        for t in range(0, 32, 2):
+            fin(t)

@@ -16,18 +16,24 @@ P = 128
 NODES = 4096
 FLOPS = 2 * (NODES * 128 * 256 + NODES * NODES * 256 + NODES * 512 * 128)
 
+ROOT = 2.0**-12
+EA = 8
+EB = 13
+JN = 1
+FPR = 2
+
 NA = 16
 LAG = 2
-R = 3
-L = 22
-X1AT = {6 + 3 * q: (q,) for q in range(8)}
+R = 4
+L = 20
+X1AT = {3 + 4 * q: (q,) for q in range(8)}
 VEM = 999
 H_RG = (1, 1)
 H_CQ = (2, 0)
 H_S3 = 3
 H_EX = (4, 2)
 WARM = 5
-SUP_HEAD = 5
+SUP_HEAD = 8
 
 
 def tile_gcn_pb_t_kernel(tc, x1, x2, adj, W3, b3, Wl, bl, out):
@@ -82,10 +88,10 @@ def tile_gcn_pb_t_kernel(tc, x1, x2, adj, W3, b3, Wl, bl, out):
             nc.sync.dma_start(out=raw[:], in_=adj_v[a])
             raws[a] = raw
 
-        load(0)
-        load(1)
-        load(2)
-        nc.sync.dma_start(out=x12[:, 0], in_=x1_v)
+        for a in range(3):
+            load(a)
+            nc.sync.dma_start(out=x12[:, 0, 4 * a:4 * a + 4], in_=x1_v[:, 4 * a:4 * a + 4])
+        nc.sync.dma_start(out=x12[:, 0, 12:16], in_=x1_v[:, 12:16])
 
         catp = const.tile([P, 4, NODES], BF16, name="catp")
         logit = const.tile([P, 32, P], F32, name="logit")
@@ -93,6 +99,9 @@ def tile_gcn_pb_t_kernel(tc, x1, x2, adj, W3, b3, Wl, bl, out):
         sums = const.tile([P, 32], F32, name="sums")
         lns = const.tile([P, 32], F32, name="lns")
         shift = const.tile([P, 32], F32, name="shift")
+        ratio = const.tile([P, 32], F32, name="ratio")
+        root = const.tile([P, 32], F32, name="root")
+        nc.vector.memset(root[:], ROOT)
         junk = const.tile([P, P], BF16, name="junk")
         b3c = const.tile([P, 2], F32, name="b3c")
         blbc = const.tile([P, P], F32, name="blbc")
@@ -172,6 +181,7 @@ def tile_gcn_pb_t_kernel(tc, x1, x2, adj, W3, b3, Wl, bl, out):
                 nc.vector.quantize_mx(out=wlc[:].bitcast(FP8X4), scales=wls[:], in_=wlg[:].rearrange("p c t -> p (c t)"))
             if g % 2 == 0 and g >= 2:
                 sup_q(g // 2 - 1)
+        sup_q(3)
 
         banks = {}
         grps = {}
@@ -287,6 +297,24 @@ def tile_gcn_pb_t_kernel(tc, x1, x2, adj, W3, b3, Wl, bl, out):
 
         def logs(t0, t1):
             nc.scalar.activation(out=lns[:, t0:t1], in_=sums[:, t0:t1], func=ACT.Ln)
+            shifts(t0, t1)
+
+        def log_guess(t0, t1):
+            nc.gpsimd.tensor_tensor(out=ratio[:, t0:t1], in0=sums[:, t0:t1], in1=root[:, t0:t1], op=ALU.pow)
+
+        def log_start(t0, t1):
+            nc.vector.tensor_scalar(
+                out=lns[:, t0:t1], in0=ratio[:, t0:t1], scalar1=-1.0, scalar2=1.0 / ROOT, op0=ALU.add, op1=ALU.mult
+            )
+
+        def log_step(t0, t1):
+            nc.scalar.activation(out=ratio[:, t0:t1], in_=lns[:, t0:t1], func=ACT.Exp, scale=-1.0)
+            nc.vector.tensor_tensor(out=ratio[:, t0:t1], in0=ratio[:, t0:t1], in1=sums[:, t0:t1], op=ALU.mult)
+            nc.vector.scalar_tensor_tensor(
+                out=lns[:, t0:t1], in0=ratio[:, t0:t1], scalar=-1.0, in1=lns[:, t0:t1], op0=ALU.add, op1=ALU.add
+            )
+
+        def shifts(t0, t1):
             nc.vector.tensor_tensor(out=shift[:, t0:t1], in0=negmax[:, t0:t1], in1=lns[:, t0:t1], op=ALU.subtract)
 
         def sub(t0, t1):
@@ -305,12 +333,19 @@ def tile_gcn_pb_t_kernel(tc, x1, x2, adj, W3, b3, Wl, bl, out):
                 in_=logit[:, t0:t1, :].rearrange("p (a e) c -> p a e c", e=2),
             )
 
-        def fin(t):
-            if t // 2 % 5 in (0, 2, 4):
-                sub(t, t + 2)
-            else:
-                sub_s(t, t + 2)
-            store(t, t + 2)
+        def fin(a, on_vector):
+            (sub if on_vector else sub_s)(2 * a, 2 * a + 2)
+            store(2 * a, 2 * a + 2)
+
+        def early(a0, a1, j0):
+            t0, t1 = 2 * a0, 2 * a1
+            hang(j0 - 1, 3, lambda: log_guess(t0, t1))
+            hang(j0 + 1, 0, lambda: log_start(t0, t1))
+            for i in range(2):
+                hang(j0 + 1 + i, 2, lambda: log_step(t0, t1))
+            hang(j0 + 2, 3, lambda: shifts(t0, t1))
+            for a in range(a0, a1):
+                hang(j0 + 3 + (a - a0) // FPR, 3, lambda a=a: fin(a, True))
 
         hung = {}
 
@@ -321,7 +356,7 @@ def tile_gcn_pb_t_kernel(tc, x1, x2, adj, W3, b3, Wl, bl, out):
         nruns = -(-len(units) // R)
         md = [0]
         ends = {}
-        for j in range(nruns + 99):
+        for j in range(nruns):
             us = units[R * j:R * j + R]
             for a, g in us:
                 T(a, (g,))
@@ -356,17 +391,50 @@ def tile_gcn_pb_t_kernel(tc, x1, x2, adj, W3, b3, Wl, bl, out):
                     X3E(a)
                     hang(j + H_RG[0], H_RG[1], lambda a=a: regroup(a))
                     hang(j + H_CQ[0], H_CQ[1], lambda a=a: catQ(a))
-                    if a < NA - 2:
+                    if a < NA - 3:
                         hang(j + H_EX[0], H_EX[1], lambda a=a: post_s(a))
+                    if a == EA - 1:
+                        early(0, EA, j + H_EX[0] + JN)
                     ends[a] = j + H_S3
             for a in list(ends):
                 if ends[a] == j:
                     S3M(a)
                     post_v(a)
-            if target == 256 and ends[NA - 1] == j:
-                break
-        for a in range(NA - 2, NA):
-            post_s(a)
-        logs(0, 32)
-        for t in range(0, 32, 2):
-            fin(t)
+        flush(0)
+        while md[0] < 16 * NA - 16:
+            M(md[0])
+            md[0] += 1
+        X3E(NA - 2)
+        for i in range(8):
+            M(16 * NA - 16 + i)
+        for j in sorted(hung):
+            if j >= nruns:
+                for i in sorted(hung[j]):
+                    for f in hung[j][i]:
+                        f()
+        log_guess(2 * EA, 2 * EB)
+        S3M(NA - 3)
+        for i in range(8, 16):
+            M(16 * NA - 16 + i)
+        regroup(NA - 2)
+        post_v(NA - 3)
+        catQ(NA - 2)
+        S3M(NA - 2)
+        X3E(NA - 1)
+        post_s(NA - 3)
+        regroup(NA - 1)
+        log_start(2 * EA, 2 * EB)
+        post_v(NA - 2)
+        catQ(NA - 1)
+        post_s(NA - 2)
+        log_step(2 * EA, 2 * EB)
+        S3M(NA - 1)
+        post_v(NA - 1)
+        log_step(2 * EA, 2 * EB)
+        post_s(NA - 1)
+        shifts(2 * EA, 2 * EB)
+        for a in range(EA, EB):
+            fin(a, True)
+        logs(2 * EB, 32)
+        for a in range(EB, NA):
+            fin(a, a % 2 == 1)

@@ -27,7 +27,7 @@ LAG = 2
 R = 4
 L = 20
 X1AT = {3 + 4 * q: (q,) for q in range(8)}
-VEM = 999
+VEM = 16
 H_RG = (1, 1)
 H_CQ = (2, 0)
 H_S3 = 3
@@ -46,7 +46,7 @@ def tile_gcn_pb_t_kernel(tc, x1, x2, adj, W3, b3, Wl, bl, out):
     with ExitStack() as ctx:
         const = ctx.enter_context(tc.tile_pool(name="const", bufs=1))
         big = ctx.enter_context(tc.tile_pool(name="big", bufs=4))
-        grp_pool = ctx.enter_context(tc.tile_pool(name="grp", bufs=6))
+        grp_pool = ctx.enter_context(tc.tile_pool(name="grp", bufs=4))
         code_pool = ctx.enter_context(tc.tile_pool(name="code", bufs=3))
         cat_pool = ctx.enter_context(tc.tile_pool(name="cat", bufs=2))
         tp = ctx.enter_context(tc.psum_pool(name="tp", bufs=6))
@@ -203,23 +203,23 @@ def tile_gcn_pb_t_kernel(tc, x1, x2, adj, W3, b3, Wl, bl, out):
                 banks[(a, g)] = ps
 
         def E(a, g, on_vector):
-            grp = grp_pool.tile([P, 1024], BF16, name="grp", align_bytes=64)
-            dst = grp[:].bitcast(F32).rearrange("p (n u) -> p n u", u=2)
+            if g % 2 == 0:
+                grps[(a, g // 2)] = grp_pool.tile([P, 2, 1024], BF16, name="grp", align_bytes=64)
+            dst = grps[(a, g // 2)][:, g % 2, :].bitcast(F32).rearrange("p (n u) -> p n u", u=2)
             src = banks[(a, g)][:].rearrange("p u n -> p n u")
             if on_vector:
                 nc.vector.tensor_copy(out=dst, in_=src)
             else:
                 nc.scalar.copy(out=dst, in_=src)
-            grps[(a, g)] = grp
 
         def Q(a, g):
             if a not in codes:
                 codes[a] = code_pool.tile([P, 8, 256], U32, name="codes", align_bytes=64)
                 scls[a] = code_pool.tile([P, 8, 256], U8, name="scls", align_bytes=64)
             nc.vector.quantize_mx(
-                out=codes[a][:, g, :].bitcast(FP8X4),
-                scales=scls[a][:, g, :],
-                in_=grps[(a, g)][:],
+                out=codes[a][:, g - 1:g + 1, :].rearrange("p g n -> p (g n)").bitcast(FP8X4),
+                scales=scls[a][:, g - 1:g + 1, :].rearrange("p g n -> p (g n)"),
+                in_=grps[(a, g // 2)][:].rearrange("p g w -> p (g w)"),
             )
 
         pend = []
@@ -227,16 +227,21 @@ def tile_gcn_pb_t_kernel(tc, x1, x2, adj, W3, b3, Wl, bl, out):
 
         def flush(keep):
             for a, g in pend[qi[0]:len(pend) - keep]:
-                Q(a, g)
+                if g % 2 == 1:
+                    Q(a, g)
             qi[0] = max(qi[0], len(pend) - keep)
 
         def M(m):
             a, h, g = m // 16, m % 16 // 8, m % 8
             if h == 0 and g == 0:
-                accs[a] = accp.tile([P, 2, 256], F32, name="acc")
+                acc = accp.tile([P, 2, 256], F32, name="acc")
+                accs[a] = (acc[:, 0, :], acc[:, 1, :])
+            if a == NA - 1 and h == 1 and g == 0:
+                acc = tp.tile([P, 256], F32, name="acc_last", tag="tp")
+                accs[a] = (accs[a][0], acc[:])
             s0 = (2 * g + h) * P
             nc.tensor.matmul_mx(
-                out=accs[a][:, h, :],
+                out=accs[a][h],
                 lhsT=supc[:, s0:s0 + P].bitcast(FP8X4),
                 lhsT_scale=sups[:, s0:s0 + P],
                 rhs=codes[a][:, g, :].bitcast(FP8X4),
@@ -245,10 +250,21 @@ def tile_gcn_pb_t_kernel(tc, x1, x2, adj, W3, b3, Wl, bl, out):
                 stop=(g == 7),
             )
 
-        def X3E(a):
+        def x3_s(a, h):
             n0 = 256 * a
-            nc.scalar.activation(out=catp[:, 2, n0:n0 + 256], in_=accs[a][:, 0, :], func=ACT.Identity, bias=b3c[:, 0:1], scale=1.0)
-            nc.vector.tensor_scalar(out=catp[:, 3, n0:n0 + 256], in0=accs[a][:, 1, :], scalar1=b3c[:, 1:2], scalar2=None, op0=ALU.add)
+            nc.scalar.activation(
+                out=catp[:, 2 + h, n0:n0 + 256], in_=accs[a][h], func=ACT.Identity, bias=b3c[:, h:h + 1], scale=1.0
+            )
+
+        def x3_v(a, h):
+            n0 = 256 * a
+            nc.vector.tensor_scalar(
+                out=catp[:, 2 + h, n0:n0 + 256], in0=accs[a][h], scalar1=b3c[:, h:h + 1], scalar2=None, op0=ALU.add
+            )
+
+        def X3E(a):
+            x3_s(a, 0)
+            x3_v(a, 1)
 
         def regroup(a):
             n0 = 256 * a
@@ -396,15 +412,17 @@ def tile_gcn_pb_t_kernel(tc, x1, x2, adj, W3, b3, Wl, bl, out):
                     if a == EA - 1:
                         early(0, EA, j + H_EX[0] + JN)
                     ends[a] = j + H_S3
+            if j == nruns - 1:
+                flush(0)
             for a in list(ends):
                 if ends[a] == j:
                     S3M(a)
                     post_v(a)
-        flush(0)
         while md[0] < 16 * NA - 16:
             M(md[0])
             md[0] += 1
-        X3E(NA - 2)
+        x3_s(NA - 2, 0)
+        x3_s(NA - 2, 1)
         for i in range(8):
             M(16 * NA - 16 + i)
         for j in sorted(hung):
@@ -413,25 +431,26 @@ def tile_gcn_pb_t_kernel(tc, x1, x2, adj, W3, b3, Wl, bl, out):
                     for f in hung[j][i]:
                         f()
         log_guess(2 * EA, 2 * EB)
-        S3M(NA - 3)
+        x3_s(NA - 1, 0)
         for i in range(8, 16):
             M(16 * NA - 16 + i)
         regroup(NA - 2)
-        post_v(NA - 3)
         catQ(NA - 2)
+        x3_s(NA - 1, 1)
+        S3M(NA - 3)
         S3M(NA - 2)
-        X3E(NA - 1)
-        post_s(NA - 3)
         regroup(NA - 1)
-        log_start(2 * EA, 2 * EB)
-        post_v(NA - 2)
+        post_v(NA - 3)
         catQ(NA - 1)
-        post_s(NA - 2)
-        log_step(2 * EA, 2 * EB)
         S3M(NA - 1)
+        post_s(NA - 3)
+        post_v(NA - 2)
+        post_s(NA - 2)
         post_v(NA - 1)
-        log_step(2 * EA, 2 * EB)
+        log_start(2 * EA, 2 * EB)
         post_s(NA - 1)
+        log_step(2 * EA, 2 * EB)
+        log_step(2 * EA, 2 * EB)
         shifts(2 * EA, 2 * EB)
         for a in range(EA, EB):
             fin(a, True)

@@ -27,7 +27,6 @@ LAG = 2
 R = 4
 L = 20
 X1AT = {3 + 4 * q: (q,) for q in range(8)}
-VEM = 16
 H_RG = (1, 1)
 H_CQ = (2, 0)
 H_S3 = 3
@@ -378,17 +377,14 @@ def tile_gcn_pb_t_kernel(tc, x1, x2, adj, W3, b3, Wl, bl, out):
                 T(a, (g,))
                 if g == 7 and a + 3 < NA:
                     load(a + 3)
-            for q in X1AT.get(j, ()):
-                feat_T(0, (q,))
             if SUP_HEAD + j < 8:
                 sup(SUP_HEAD + j)
             pieces = hung.get(j, {})
-            if not us:
-                flush(0)
+            pieces.setdefault(R // 2, []).extend([lambda q=q: feat_T(0, (q,)) for q in X1AT.get(j, ())])
             for i in range(max(R, 4)):
                 if i < len(us):
                     a, g = us[i]
-                    E(a, g, (R * j + i) % VEM == 1 and j >= 6)
+                    E(a, g, (R * j + i) % 8 == 1 and 6 <= j < 24)
                     pend.append((a, g))
                     flush(LAG)
                 for f in pieces.get(i, []):

@@ -101,7 +101,7 @@ def tile_gcn_pb_t_kernel(tc, x1, x2, adj, W3, b3, Wl, bl, out):
         ratio = const.tile([P, 32], F32, name="ratio")
         root = const.tile([P, 32], F32, name="root")
         nc.vector.memset(root[:], ROOT)
-        junk = const.tile([P, P], BF16, name="junk")
+        junk = const.tile([P, 2, P], BF16, name="junk")
         b3c = const.tile([P, 2], F32, name="b3c")
         blbc = const.tile([P, P], F32, name="blbc")
         supc = const.tile([P, 16 * P], U32, name="supc", align_bytes=64)
@@ -294,15 +294,19 @@ def tile_gcn_pb_t_kernel(tc, x1, x2, adj, W3, b3, Wl, bl, out):
                     stop=True,
                 )
 
-        def post_v(a):
-            lb = logit[:, 2 * a:2 * a + 2, :]
-            nc.vector.tensor_tensor(out=lb, in0=lgs[a][:], in1=blbc[:].unsqueeze(1).to_broadcast([P, 2, P]), op=ALU.add)
-            nc.vector.tensor_reduce(out=negmax[:, 2 * a:2 * a + 2], in_=lb, axis=AX.X, op=ALU.max, negate=True)
+        def add_bl(a):
+            bias = blbc[:].unsqueeze(1).to_broadcast([P, 2, P])
+            nc.vector.tensor_tensor(out=logit[:, 2 * a:2 * a + 2, :], in0=lgs[a][:], in1=bias, op=ALU.add)
+
+        def row_max(a):
+            nc.vector.tensor_reduce(
+                out=negmax[:, 2 * a:2 * a + 2], in_=logit[:, 2 * a:2 * a + 2, :], axis=AX.X, op=ALU.max, negate=True
+            )
 
         def post_s(a):
             for t in range(2 * a, 2 * a + 2):
                 nc.scalar.activation(
-                    out=junk[:],
+                    out=junk[:, t % 2, :],
                     in_=logit[:, t, :],
                     func=ACT.Exp,
                     bias=negmax[:, t:t + 1],
@@ -322,9 +326,13 @@ def tile_gcn_pb_t_kernel(tc, x1, x2, adj, W3, b3, Wl, bl, out):
                 out=lns[:, t0:t1], in0=ratio[:, t0:t1], scalar1=-1.0, scalar2=1.0 / ROOT, op0=ALU.add, op1=ALU.mult
             )
 
-        def log_step(t0, t1):
+        def log_step_s(t0, t1):
             nc.scalar.activation(out=ratio[:, t0:t1], in_=lns[:, t0:t1], func=ACT.Exp, scale=-1.0)
+
+        def log_mul(t0, t1):
             nc.vector.tensor_tensor(out=ratio[:, t0:t1], in0=ratio[:, t0:t1], in1=sums[:, t0:t1], op=ALU.mult)
+
+        def log_add(t0, t1):
             nc.vector.scalar_tensor_tensor(
                 out=lns[:, t0:t1], in0=ratio[:, t0:t1], scalar=-1.0, in1=lns[:, t0:t1], op0=ALU.add, op1=ALU.add
             )
@@ -357,8 +365,10 @@ def tile_gcn_pb_t_kernel(tc, x1, x2, adj, W3, b3, Wl, bl, out):
             hang(j0 - 1, 3, lambda: log_guess(t0, t1))
             hang(j0 + 1, 0, lambda: log_start(t0, t1))
             for i in range(2):
-                hang(j0 + 1 + i, 2, lambda: log_step(t0, t1))
-            hang(j0 + 2, 3, lambda: shifts(t0, t1))
+                hang(j0 + 1 + i, 1, lambda: log_step_s(t0, t1))
+                hang(j0 + 1 + i, 2, lambda: log_mul(t0, t1))
+                hang(j0 + 1 + i, 3, lambda: log_add(t0, t1))
+            hang(j0 + 3, 0, lambda: shifts(t0, t1))
             for a in range(a0, a1):
                 hang(j0 + 3 + (a - a0) // FPR, 3, lambda a=a: fin(a, True))
 
@@ -413,7 +423,8 @@ def tile_gcn_pb_t_kernel(tc, x1, x2, adj, W3, b3, Wl, bl, out):
             for a in list(ends):
                 if ends[a] == j:
                     S3M(a)
-                    post_v(a)
+                    add_bl(a)
+                    hang(j + 1, 0, lambda a=a: row_max(a))
         while md[0] < 16 * NA - 16:
             M(md[0])
             md[0] += 1
@@ -431,22 +442,29 @@ def tile_gcn_pb_t_kernel(tc, x1, x2, adj, W3, b3, Wl, bl, out):
         for i in range(8, 16):
             M(16 * NA - 16 + i)
         regroup(NA - 2)
-        catQ(NA - 2)
         x3_s(NA - 1, 1)
         S3M(NA - 3)
+        add_bl(NA - 3)
+        catQ(NA - 2)
         S3M(NA - 2)
         regroup(NA - 1)
-        post_v(NA - 3)
+        row_max(NA - 3)
         catQ(NA - 1)
+        add_bl(NA - 2)
         S3M(NA - 1)
         post_s(NA - 3)
-        post_v(NA - 2)
-        post_s(NA - 2)
-        post_v(NA - 1)
+        row_max(NA - 2)
+        add_bl(NA - 1)
         log_start(2 * EA, 2 * EB)
+        row_max(NA - 1)
+        post_s(NA - 2)
+        log_step_s(2 * EA, 2 * EB)
+        log_mul(2 * EA, 2 * EB)
+        log_add(2 * EA, 2 * EB)
         post_s(NA - 1)
-        log_step(2 * EA, 2 * EB)
-        log_step(2 * EA, 2 * EB)
+        log_step_s(2 * EA, 2 * EB)
+        log_mul(2 * EA, 2 * EB)
+        log_add(2 * EA, 2 * EB)
         shifts(2 * EA, 2 * EB)
         for a in range(EA, EB):
             fin(a, True)

@@ -83,7 +83,7 @@ def tile_gcn_pb_t_kernel(tc, x1, x2, adj, W3, b3, Wl, bl, out):
         raws = {}
 
         def load(a):
-            raw = big.tile([P, 2, NODES], BF16, name="raw", tag="big", align_bytes=64)
+            raw = big.tile([P, 2, NODES], BF16, name="raw", tag="big", align_bytes=256)
             nc.sync.dma_start(out=raw[:], in_=adj_v[a])
             raws[a] = raw
 
@@ -104,11 +104,11 @@ def tile_gcn_pb_t_kernel(tc, x1, x2, adj, W3, b3, Wl, bl, out):
         junk = const.tile([P, 2, P], BF16, name="junk")
         b3c = const.tile([P, 2], F32, name="b3c")
         blbc = const.tile([P, P], F32, name="blbc")
-        supc = const.tile([P, 16 * P], U32, name="supc", align_bytes=64)
-        sups = const.tile([P, 16 * P], U8, name="sups", align_bytes=64)
-        wlg = const.tile([P, P, 4], BF16, name="wlg", align_bytes=64)
-        wlc = const.tile([P, P], U32, name="wlc", align_bytes=64)
-        wls = const.tile([P, P], U8, name="wls", align_bytes=64)
+        supc = const.tile([P, 16 * P], U32, name="supc", align_bytes=256)
+        sups = const.tile([P, 16 * P], U8, name="sups", align_bytes=256)
+        wlg = const.tile([P, P, 4], BF16, name="wlg", align_bytes=256)
+        wlc = const.tile([P, P], U32, name="wlc", align_bytes=256)
+        wls = const.tile([P, P], U8, name="wls", align_bytes=256)
 
         flip = [0]
 
@@ -147,7 +147,7 @@ def tile_gcn_pb_t_kernel(tc, x1, x2, adj, W3, b3, Wl, bl, out):
             in_=wl_sb[:].rearrange("p t (c i) -> p c t i", i=4),
         )
 
-        supg = big.tile([P, 16, 512], BF16, name="supg", tag="big", align_bytes=64)
+        supg = big.tile([P, 16, 512], BF16, name="supg", tag="big", align_bytes=256)
 
         def sup_q(q):
             nc.vector.quantize_mx(
@@ -203,7 +203,7 @@ def tile_gcn_pb_t_kernel(tc, x1, x2, adj, W3, b3, Wl, bl, out):
 
         def E(a, g, on_vector):
             if g % 2 == 0:
-                grps[(a, g // 2)] = grp_pool.tile([P, 2, 1024], BF16, name="grp", align_bytes=64)
+                grps[(a, g // 2)] = grp_pool.tile([P, 2, 1024], BF16, name="grp", align_bytes=256)
             dst = grps[(a, g // 2)][:, g % 2, :].bitcast(F32).rearrange("p (n u) -> p n u", u=2)
             src = banks[(a, g)][:].rearrange("p u n -> p n u")
             if on_vector:
@@ -213,8 +213,8 @@ def tile_gcn_pb_t_kernel(tc, x1, x2, adj, W3, b3, Wl, bl, out):
 
         def Q(a, g):
             if a not in codes:
-                codes[a] = code_pool.tile([P, 8, 256], U32, name="codes", align_bytes=64)
-                scls[a] = code_pool.tile([P, 8, 256], U8, name="scls", align_bytes=64)
+                codes[a] = code_pool.tile([P, 8, 256], U32, name="codes", align_bytes=256)
+                scls[a] = code_pool.tile([P, 8, 256], U8, name="scls", align_bytes=256)
             nc.vector.quantize_mx(
                 out=codes[a][:, g - 1:g + 1, :].rearrange("p g n -> p (g n)").bitcast(FP8X4),
                 scales=scls[a][:, g - 1:g + 1, :].rearrange("p g n -> p (g n)"),
@@ -267,7 +267,7 @@ def tile_gcn_pb_t_kernel(tc, x1, x2, adj, W3, b3, Wl, bl, out):
 
         def regroup(a):
             n0 = 256 * a
-            catg = cat_pool.tile([P, 256, 4], BF16, name="catg", align_bytes=64)
+            catg = cat_pool.tile([P, 256, 4], BF16, name="catg", align_bytes=256)
             nc.vector.tensor_copy(
                 out=catg[:].rearrange("p (c i) t -> p c t i", i=4),
                 in_=catp[:, :, n0:n0 + 256].rearrange("p t (c i) -> p c t i", i=4),
@@ -275,8 +275,8 @@ def tile_gcn_pb_t_kernel(tc, x1, x2, adj, W3, b3, Wl, bl, out):
             catgs[a] = catg
 
         def catQ(a):
-            catc = cat_pool.tile([P, 256], U32, name="catc", align_bytes=64)
-            cats = cat_pool.tile([P, 256], U8, name="cats", align_bytes=64)
+            catc = cat_pool.tile([P, 256], U32, name="catc", align_bytes=256)
+            cats = cat_pool.tile([P, 256], U8, name="cats", align_bytes=256)
             nc.vector.quantize_mx(out=catc[:].bitcast(FP8X4), scales=cats[:], in_=catgs[a][:].rearrange("p n t -> p (n t)"))
             catcs[a] = (catc, cats)
 
@@ -439,18 +439,20 @@ def tile_gcn_pb_t_kernel(tc, x1, x2, adj, W3, b3, Wl, bl, out):
                         f()
         log_guess(2 * EA, 2 * EB)
         x3_s(NA - 1, 0)
-        for i in range(8, 16):
-            M(16 * NA - 16 + i)
         regroup(NA - 2)
-        x3_s(NA - 1, 1)
+        for i in range(8, 12):
+            M(16 * NA - 16 + i)
         S3M(NA - 3)
+        for i in range(12, 16):
+            M(16 * NA - 16 + i)
+        x3_s(NA - 1, 1)
         add_bl(NA - 3)
         catQ(NA - 2)
+        row_max(NA - 3)
         S3M(NA - 2)
         regroup(NA - 1)
-        row_max(NA - 3)
-        catQ(NA - 1)
         add_bl(NA - 2)
+        catQ(NA - 1)
         S3M(NA - 1)
         post_s(NA - 3)
         row_max(NA - 2)

@@ -84,13 +84,19 @@ def tile_gcn_pb_t_kernel(tc, x1, x2, adj, W3, b3, Wl, bl, out):
 
         def load(a):
             raw = big.tile([P, 2, NODES], BF16, name="raw", tag="big", align_bytes=256)
-            nc.sync.dma_start(out=raw[:], in_=adj_v[a])
+            parts = 2 if a < 4 else 1
+            for i in range(parts):
+                c0, c1 = NODES // parts * i, NODES // parts * (i + 1)
+                nc.sync.dma_start(out=raw[:, :, c0:c1], in_=adj_v[a, :, :, c0:c1])
             raws[a] = raw
 
-        for a in range(3):
-            load(a)
-            nc.sync.dma_start(out=x12[:, 0, 4 * a:4 * a + 4], in_=x1_v[:, 4 * a:4 * a + 4])
-        nc.sync.dma_start(out=x12[:, 0, 12:16], in_=x1_v[:, 12:16])
+        def load_x1(q):
+            nc.sync.dma_start(out=x12[:, 0, 4 * q:4 * q + 4], in_=x1_v[:, 4 * q:4 * q + 4])
+
+        load(0)
+        load(1)
+        load_x1(0)
+        load(2)
 
         catp = const.tile([P, 4, NODES], BF16, name="catp")
         logit = const.tile([P, 32, P], F32, name="logit")
@@ -387,6 +393,8 @@ def tile_gcn_pb_t_kernel(tc, x1, x2, adj, W3, b3, Wl, bl, out):
                 T(a, (g,))
                 if g == 7 and a + 3 < NA:
                     load(a + 3)
+                    if a % 4 == 2 and a < 12:
+                        load_x1(a // 4 + 1)
             if SUP_HEAD + j < 8:
                 sup(SUP_HEAD + j)
             pieces = hung.get(j, {})

@@ -84,10 +84,7 @@ def tile_gcn_pb_t_kernel(tc, x1, x2, adj, W3, b3, Wl, bl, out):
 
         def load(a):
             raw = big.tile([P, 2, NODES], BF16, name="raw", tag="big", align_bytes=256)
-            parts = 2 if a < 4 else 1
-            for i in range(parts):
-                c0, c1 = NODES // parts * i, NODES // parts * (i + 1)
-                nc.sync.dma_start(out=raw[:, :, c0:c1], in_=adj_v[a, :, :, c0:c1])
+            nc.sync.dma_start(out=raw[:], in_=adj_v[a])
             raws[a] = raw
 
         def load_x1(q):

from contextlib import ExitStack

import concourse.mybir as mybir
from concourse.masks import make_identity

F32 = mybir.dt.float32
BF16 = mybir.dt.bfloat16
U32 = mybir.dt.uint32
U8 = mybir.dt.uint8
FP8X4 = mybir.dt.float8_e4m3fn_x4
ACT = mybir.ActivationFunctionType
ALU = mybir.AluOpType
AX = mybir.AxisListType

P = 128
NODES = 4096
FLOPS = 2 * (NODES * 128 * 256 + NODES * NODES * 256 + NODES * 512 * 128)

ROOT = 2.0**-12
EA = 8
EB = 13
JN = 1
FPR = 2

NA = 16
LAG = 2
R = 4
L = 20
X1AT = {3 + 4 * q: (q,) for q in range(8)}
H_RG = (1, 1)
H_CQ = (2, 0)
H_S3 = 3
H_EX = (4, 2)
WARM = 5
SUP_HEAD = 8


def tile_gcn_pb_t_kernel(tc, x1, x2, adj, W3, b3, Wl, bl, out):
    nc = tc.nc
    adj_v = adj.rearrange("(a p e) j -> a p e j", p=P, e=2)
    x1_v = x1.rearrange("(a p e) f -> p a e f", p=P, e=2)
    x2_v = x2.rearrange("(a p e) f -> p a e f", p=P, e=2)
    out_v = out.rearrange("(a p e) c -> p a e c", p=P, e=2)

    with ExitStack() as ctx:
        const = ctx.enter_context(tc.tile_pool(name="const", bufs=1))
        big = ctx.enter_context(tc.tile_pool(name="big", bufs=4))
        grp_pool = ctx.enter_context(tc.tile_pool(name="grp", bufs=4))
        code_pool = ctx.enter_context(tc.tile_pool(name="code", bufs=3))
        cat_pool = ctx.enter_context(tc.tile_pool(name="cat", bufs=2))
        tp = ctx.enter_context(tc.psum_pool(name="tp", bufs=6))
        accp = ctx.enter_context(tc.psum_pool(name="accp", bufs=2))
        ctx.enter_context(tc.manual_schedule())

        zb = const.tile([P, P], BF16, name="zb")
        yb = const.tile([P, P], BF16, name="yb")
        ones = const.tile([P, P], BF16, name="ones")
        dm = const.tile([P, 1], F32, name="dm")
        dm2 = const.tile([P, 1], F32, name="dm2")
        warm = const.tile([P, 512], BF16, name="warm")
        nc.vector.memset(warm[:], 0.0)
        nc.vector.memset(zb[:], 0.0)
        nc.vector.memset(yb[:], 0.0)
        nc.vector.memset(ones[:], 1.0)
        nc.vector.memset(dm[:], 0.0)
        ident_b = const.tile([P, P], BF16, name="ident_b")
        ident_f = const.tile([P, P], F32, name="ident_f")
        make_identity(nc, ident_b[:])
        make_identity(nc, ident_f[:])

        wl_sb = const.tile([P, 4, P], BF16, name="wl_sb")
        nc.scalar.dma_start(out=wl_sb[:], in_=Wl.rearrange("(t p) c -> p t c", p=P))
        nc.scalar.dma_start(out=yb[0:2, :], in_=b3.rearrange("(h p) -> h p", h=2))
        nc.scalar.dma_start(out=zb[0:1, :], in_=bl.rearrange("(o c) -> o c", o=1))
        nc.scalar.activation(out=dm2[:], in_=dm[:], func=ACT.Exp)

        w3 = const.tile([P, 256], BF16, name="w3")
        nc.sync.dma_start(out=w3[:], in_=W3)
        x12 = const.tile([P, 2, 16, 2, P], BF16, name="x12")
        for q in range(4):
            nc.sync.dma_start(out=x12[:, 1, 4 * q:4 * q + 4], in_=x2_v[:, 4 * q:4 * q + 4])

        raws = {}

        def load(a):
            raw = big.tile([P, 2, NODES], BF16, name="raw", tag="big", align_bytes=256)
            nc.sync.dma_start(out=raw[:], in_=adj_v[a])
            raws[a] = raw

        def load_x1(q):
            nc.sync.dma_start(out=x12[:, 0, 4 * q:4 * q + 4], in_=x1_v[:, 4 * q:4 * q + 4])

        load(0)
        load(1)
        load_x1(0)
        load(2)

        catp = const.tile([P, 4, NODES], BF16, name="catp")
        logit = const.tile([P, 32, P], F32, name="logit")
        negmax = const.tile([P, 32], F32, name="negmax")
        sums = const.tile([P, 32], F32, name="sums")
        lns = const.tile([P, 32], F32, name="lns")
        shift = const.tile([P, 32], F32, name="shift")
        ratio = const.tile([P, 32], F32, name="ratio")
        root = const.tile([P, 32], F32, name="root")
        nc.vector.memset(root[:], ROOT)
        junk = const.tile([P, 2, P], BF16, name="junk")
        b3c = const.tile([P, 2], F32, name="b3c")
        blbc = const.tile([P, P], F32, name="blbc")
        supc = const.tile([P, 16 * P], U32, name="supc", align_bytes=256)
        sups = const.tile([P, 16 * P], U8, name="sups", align_bytes=256)
        wlg = const.tile([P, P, 4], BF16, name="wlg", align_bytes=256)
        wlc = const.tile([P, P], U32, name="wlc", align_bytes=256)
        wls = const.tile([P, P], U8, name="wls", align_bytes=256)

        flip = [0]

        def copy_alt(dst, src):
            flip[0] ^= 1
            if flip[0]:
                nc.scalar.copy(out=dst, in_=src)
            else:
                nc.vector.tensor_copy(out=dst, in_=src)

        def feat_T(plane, qs):
            for q in qs:
                ps = tp.tile([P, 4, P], BF16, name="ps_x", tag="tp")
                for j in range(4):
                    tau = 4 * q + j
                    nc.tensor.transpose(ps[:, j, :], x12[:, plane, tau // 2, tau % 2, :], ident_b[:])
                copy_alt(catp[:, plane, 512 * q:512 * q + 512], ps[:].rearrange("p j n -> p (j n)"))

        def dummy(n):
            ps = tp.tile([P, 512], F32, name="ps_d", tag="tp")
            for i in range(n):
                nc.tensor.matmul(ps[:], lhsT=warm[:, 0:P], rhs=warm[:], start=True, stop=True)

        dummy(WARM)
        feat_T(1, range(2))

        psb = tp.tile([P, P], BF16, name="psb", tag="tp")
        nc.tensor.transpose(psb[:], yb[:], ident_b[:])
        nc.vector.tensor_copy(out=b3c[:], in_=psb[:, 0:2])
        psl = tp.tile([P, P], F32, name="psl", tag="tp")
        nc.tensor.matmul(psl[:], lhsT=ones[:], rhs=zb[:], start=True, stop=True)
        nc.vector.tensor_copy(out=blbc[:], in_=psl[:])

        nc.vector.tensor_copy(
            out=wlg[:].rearrange("p (c i) t -> p c t i", i=4),
            in_=wl_sb[:].rearrange("p t (c i) -> p c t i", i=4),
        )

        supg = big.tile([P, 16, 512], BF16, name="supg", tag="big", align_bytes=256)

        def sup_q(q):
            nc.vector.quantize_mx(
                out=supc[:, 512 * q:512 * q + 512].bitcast(FP8X4),
                scales=sups[:, 512 * q:512 * q + 512],
                in_=supg[:, 4 * q:4 * q + 4, :].rearrange("p s w -> p (s w)"),
            )

        def sup(g):
            for h in range(2):
                ps = tp.tile([P, 4, P], F32, name="ps_s", tag="tp")
                for t in range(4):
                    nc.tensor.matmul(
                        ps[:, t, :],
                        lhsT=catp[:, 1, (4 * g + t) * P:(4 * g + t + 1) * P],
                        rhs=w3[:, h * P:(h + 1) * P],
                        start=True,
                        stop=True,
                    )
                (copy_alt if g < SUP_HEAD else nc.vector.tensor_copy)(
                    supg[:, 2 * g + h, :].rearrange("p (c t) -> p c t", t=4),
                    ps[:].rearrange("p t c -> p c t"),
                )

        for g in range(SUP_HEAD):
            sup(g)
            if g < 3:
                feat_T(1, range(2 + 2 * g, 4 + 2 * g))
            if g == 0:
                nc.vector.quantize_mx(out=wlc[:].bitcast(FP8X4), scales=wls[:], in_=wlg[:].rearrange("p c t -> p (c t)"))
            if g % 2 == 0 and g >= 2:
                sup_q(g // 2 - 1)
        sup_q(3)

        banks = {}
        grps = {}
        codes = {}
        scls = {}
        accs = {}
        catgs = {}
        catcs = {}
        lgs = {}

        def T(a, gs):
            rawf = raws[a][:].bitcast(F32)
            for g in gs:
                ps = tp.tile([P, 2, 256], F32, name="ps_t", tag="tp")
                for u in range(2):
                    for e in range(2):
                        w0 = 256 * g + 128 * u
                        nc.tensor.transpose(ps[:, u, e * P:(e + 1) * P], rawf[:, e, w0:w0 + P], ident_f[:])
                banks[(a, g)] = ps

        def E(a, g, on_vector):
            if g % 2 == 0:
                grps[(a, g // 2)] = grp_pool.tile([P, 2, 1024], BF16, name="grp", align_bytes=256)
            dst = grps[(a, g // 2)][:, g % 2, :].bitcast(F32).rearrange("p (n u) -> p n u", u=2)
            src = banks[(a, g)][:].rearrange("p u n -> p n u")
            if on_vector:
                nc.vector.tensor_copy(out=dst, in_=src)
            else:
                nc.scalar.copy(out=dst, in_=src)

        def Q(a, g):
            if a not in codes:
                codes[a] = code_pool.tile([P, 8, 256], U32, name="codes", align_bytes=256)
                scls[a] = code_pool.tile([P, 8, 256], U8, name="scls", align_bytes=256)
            nc.vector.quantize_mx(
                out=codes[a][:, g - 1:g + 1, :].rearrange("p g n -> p (g n)").bitcast(FP8X4),
                scales=scls[a][:, g - 1:g + 1, :].rearrange("p g n -> p (g n)"),
                in_=grps[(a, g // 2)][:].rearrange("p g w -> p (g w)"),
            )

        pend = []
        qi = [0]

        def flush(keep):
            for a, g in pend[qi[0]:len(pend) - keep]:
                if g % 2 == 1:
                    Q(a, g)
            qi[0] = max(qi[0], len(pend) - keep)

        def M(m):
            a, h, g = m // 16, m % 16 // 8, m % 8
            if h == 0 and g == 0:
                acc = accp.tile([P, 2, 256], F32, name="acc")
                accs[a] = (acc[:, 0, :], acc[:, 1, :])
            if a == NA - 1 and h == 1 and g == 0:
                acc = tp.tile([P, 256], F32, name="acc_last", tag="tp")
                accs[a] = (accs[a][0], acc[:])
            s0 = (2 * g + h) * P
            nc.tensor.matmul_mx(
                out=accs[a][h],
                lhsT=supc[:, s0:s0 + P].bitcast(FP8X4),
                lhsT_scale=sups[:, s0:s0 + P],
                rhs=codes[a][:, g, :].bitcast(FP8X4),
                rhs_scale=scls[a][:, g, :],
                start=(g == 0),
                stop=(g == 7),
            )

        def x3_s(a, h):
            n0 = 256 * a
            nc.scalar.activation(
                out=catp[:, 2 + h, n0:n0 + 256], in_=accs[a][h], func=ACT.Identity, bias=b3c[:, h:h + 1], scale=1.0
            )

        def x3_v(a, h):
            n0 = 256 * a
            nc.vector.tensor_scalar(
                out=catp[:, 2 + h, n0:n0 + 256], in0=accs[a][h], scalar1=b3c[:, h:h + 1], scalar2=None, op0=ALU.add
            )

        def X3E(a):
            x3_s(a, 0)
            x3_v(a, 1)

        def regroup(a):
            n0 = 256 * a
            catg = cat_pool.tile([P, 256, 4], BF16, name="catg", align_bytes=256)
            nc.vector.tensor_copy(
                out=catg[:].rearrange("p (c i) t -> p c t i", i=4),
                in_=catp[:, :, n0:n0 + 256].rearrange("p t (c i) -> p c t i", i=4),
            )
            catgs[a] = catg

        def catQ(a):
            catc = cat_pool.tile([P, 256], U32, name="catc", align_bytes=256)
            cats = cat_pool.tile([P, 256], U8, name="cats", align_bytes=256)
            nc.vector.quantize_mx(out=catc[:].bitcast(FP8X4), scales=cats[:], in_=catgs[a][:].rearrange("p n t -> p (n t)"))
            catcs[a] = (catc, cats)

        def S3M(a):
            catc, cats = catcs[a]
            lgs[a] = tp.tile([P, 2, P], F32, name="lg", tag="tp")
            for j in range(2):
                nc.tensor.matmul_mx(
                    out=lgs[a][:, j, :],
                    lhsT=catc[:, j * P:(j + 1) * P].bitcast(FP8X4),
                    lhsT_scale=cats[:, j * P:(j + 1) * P],
                    rhs=wlc[:].bitcast(FP8X4),
                    rhs_scale=wls[:],
                    start=True,
                    stop=True,
                )

        def add_bl(a):
            bias = blbc[:].unsqueeze(1).to_broadcast([P, 2, P])
            nc.vector.tensor_tensor(out=logit[:, 2 * a:2 * a + 2, :], in0=lgs[a][:], in1=bias, op=ALU.add)

        def row_max(a):
            nc.vector.tensor_reduce(
                out=negmax[:, 2 * a:2 * a + 2], in_=logit[:, 2 * a:2 * a + 2, :], axis=AX.X, op=ALU.max, negate=True
            )

        def post_s(a):
            for t in range(2 * a, 2 * a + 2):
                nc.scalar.activation(
                    out=junk[:, t % 2, :],
                    in_=logit[:, t, :],
                    func=ACT.Exp,
                    bias=negmax[:, t:t + 1],
                    scale=1.0,
                    accum_out=sums[:, t:t + 1],
                )

        def logs(t0, t1):
            nc.scalar.activation(out=lns[:, t0:t1], in_=sums[:, t0:t1], func=ACT.Ln)
            shifts(t0, t1)

        def log_guess(t0, t1):
            nc.gpsimd.tensor_tensor(out=ratio[:, t0:t1], in0=sums[:, t0:t1], in1=root[:, t0:t1], op=ALU.pow)

        def log_start(t0, t1):
            nc.vector.tensor_scalar(
                out=lns[:, t0:t1], in0=ratio[:, t0:t1], scalar1=-1.0, scalar2=1.0 / ROOT, op0=ALU.add, op1=ALU.mult
            )

        def log_step_s(t0, t1):
            nc.scalar.activation(out=ratio[:, t0:t1], in_=lns[:, t0:t1], func=ACT.Exp, scale=-1.0)

        def log_mul(t0, t1):
            nc.vector.tensor_tensor(out=ratio[:, t0:t1], in0=ratio[:, t0:t1], in1=sums[:, t0:t1], op=ALU.mult)

        def log_add(t0, t1):
            nc.vector.scalar_tensor_tensor(
                out=lns[:, t0:t1], in0=ratio[:, t0:t1], scalar=-1.0, in1=lns[:, t0:t1], op0=ALU.add, op1=ALU.add
            )

        def shifts(t0, t1):
            nc.vector.tensor_tensor(out=shift[:, t0:t1], in0=negmax[:, t0:t1], in1=lns[:, t0:t1], op=ALU.subtract)

        def sub(t0, t1):
            for t in range(t0, t1):
                nc.vector.tensor_scalar(
                    out=logit[:, t, :], in0=logit[:, t, :], scalar1=shift[:, t:t + 1], scalar2=None, op0=ALU.add
                )

        def sub_s(t0, t1):
            for t in range(t0, t1):
                nc.scalar.activation(out=logit[:, t, :], in_=logit[:, t, :], func=ACT.Identity, bias=shift[:, t:t + 1], scale=1.0)

        def store(t0, t1):
            nc.sync.dma_start(
                out=out_v[:, t0 // 2:t1 // 2],
                in_=logit[:, t0:t1, :].rearrange("p (a e) c -> p a e c", e=2),
            )

        def fin(a, on_vector):
            (sub if on_vector else sub_s)(2 * a, 2 * a + 2)
            store(2 * a, 2 * a + 2)

        def early(a0, a1, j0):
            t0, t1 = 2 * a0, 2 * a1
            hang(j0 - 1, 3, lambda: log_guess(t0, t1))
            hang(j0 + 1, 0, lambda: log_start(t0, t1))
            for i in range(2):
                hang(j0 + 1 + i, 1, lambda: log_step_s(t0, t1))
                hang(j0 + 1 + i, 2, lambda: log_mul(t0, t1))
                hang(j0 + 1 + i, 3, lambda: log_add(t0, t1))
            hang(j0 + 3, 0, lambda: shifts(t0, t1))
            for a in range(a0, a1):
                hang(j0 + 3 + (a - a0) // FPR, 3, lambda a=a: fin(a, True))

        hung = {}

        def hang(r, i, f):
            hung.setdefault(r, {}).setdefault(i, []).append(f)

        units = [(a, g) for a in range(NA) for g in range(8)]
        nruns = -(-len(units) // R)
        md = [0]
        ends = {}
        for j in range(nruns):
            us = units[R * j:R * j + R]
            for a, g in us:
                T(a, (g,))
                if g == 7 and a + 3 < NA:
                    load(a + 3)
                    if a % 4 == 2 and a < 12:
                        load_x1(a // 4 + 1)
            if SUP_HEAD + j < 8:
                sup(SUP_HEAD + j)
            pieces = hung.get(j, {})
            pieces.setdefault(R // 2, []).extend([lambda q=q: feat_T(0, (q,)) for q in X1AT.get(j, ())])
            for i in range(max(R, 4)):
                if i < len(us):
                    a, g = us[i]
                    E(a, g, (R * j + i) % 8 == 1 and 6 <= j < 24)
                    pend.append((a, g))
                    flush(LAG)
                for f in pieces.get(i, []):
                    f()
            if SUP_HEAD + j == 6:
                sup_q(2)
            if SUP_HEAD + j == 7:
                sup_q(3)
            target = min(256, 2 * R * (j + 1) - L)
            while md[0] < target:
                m = md[0]
                M(m)
                md[0] += 1
                if m % 16 == 15:
                    a = m // 16
                    X3E(a)
                    hang(j + H_RG[0], H_RG[1], lambda a=a: regroup(a))
                    hang(j + H_CQ[0], H_CQ[1], lambda a=a: catQ(a))
                    if a < NA - 3:
                        hang(j + H_EX[0], H_EX[1], lambda a=a: post_s(a))
                    if a == EA - 1:
                        early(0, EA, j + H_EX[0] + JN)
                    ends[a] = j + H_S3
            if j == nruns - 1:
                flush(0)
            for a in list(ends):
                if ends[a] == j:
                    S3M(a)
                    add_bl(a)
                    hang(j + 1, 0, lambda a=a: row_max(a))
        while md[0] < 16 * NA - 16:
            M(md[0])
            md[0] += 1
        x3_s(NA - 2, 0)
        x3_s(NA - 2, 1)
        for i in range(8):
            M(16 * NA - 16 + i)
        for j in sorted(hung):
            if j >= nruns:
                for i in sorted(hung[j]):
                    for f in hung[j][i]:
                        f()
        log_guess(2 * EA, 2 * EB)
        x3_s(NA - 1, 0)
        regroup(NA - 2)
        for i in range(8, 12):
            M(16 * NA - 16 + i)
        S3M(NA - 3)
        for i in range(12, 16):
            M(16 * NA - 16 + i)
        x3_s(NA - 1, 1)
        add_bl(NA - 3)
        catQ(NA - 2)
        row_max(NA - 3)
        S3M(NA - 2)
        regroup(NA - 1)
        add_bl(NA - 2)
        catQ(NA - 1)
        S3M(NA - 1)
        post_s(NA - 3)
        row_max(NA - 2)
        add_bl(NA - 1)
        log_start(2 * EA, 2 * EB)
        row_max(NA - 1)
        post_s(NA - 2)
        log_step_s(2 * EA, 2 * EB)
        log_mul(2 * EA, 2 * EB)
        log_add(2 * EA, 2 * EB)
        post_s(NA - 1)
        log_step_s(2 * EA, 2 * EB)
        log_mul(2 * EA, 2 * EB)
        log_add(2 * EA, 2 * EB)
        shifts(2 * EA, 2 * EB)
        for a in range(EA, EB):
            fin(a, True)
        logs(2 * EB, 32)
        for a in range(EB, NA):
            fin(a, a % 2 == 1)
